import numpy as np
import ml_dtypes


def mxq(x, axis, fmt="e4m3"):
    dtype, down = {"e4m3": (ml_dtypes.float8_e4m3fn, 7), "e5m2": (ml_dtypes.float8_e5m2, 14)}[fmt]
    v = np.moveaxis(np.asarray(x, np.float32).astype(ml_dtypes.bfloat16).astype(np.float64), axis, -1)
    blocks = v.reshape(v.shape[:-1] + (-1, 32))
    amax = np.abs(blocks).max(-1, keepdims=True)
    byte = np.maximum(np.where(amax > 0, np.frexp(amax)[1] - 1 + 127, 0) - down, 1)
    scale = np.exp2(byte - 127.0)
    codes = (blocks / scale).astype(np.float32).astype(dtype).astype(np.float64)
    return np.moveaxis((codes * scale).reshape(v.shape), -1, axis)


BF16 = ml_dtypes.bfloat16


def bf(x):
    return np.asarray(x, np.float32).astype(BF16)


def f64(x):
    return np.asarray(x).astype(np.float64)


N, D, Q, CLIP, R = 1024, 1024, 256, 8, 16
EPS = 1e-6
MIX = 0.7
SELF = 6.0


def setup_inputs():
    shots = np.repeat(np.random.standard_normal((R, D)), N // R, axis=0)
    return {"frame_embeddings": bf(MIX * shots + MIX * np.random.standard_normal((N, D))),
            "tau_global_prime": bf(-np.log(SELF * np.sqrt(D)) + 0.1 * np.random.standard_normal(1))}


def reference(frame_embeddings, tau_global_prime):
    f = f64(frame_embeddings)
    tau_g = np.exp(f64(tau_global_prime))[0]
    nf = f / (np.sqrt((f * f).sum(-1, keepdims=True)) + EPS)
    nfq = mxq(nf, 1, "e4m3")
    s = (nfq @ nfq.T) / (tau_g * np.sqrt(D))
    e = np.exp(s - s.max(-1, keepdims=True))
    return (mxq(e, 1, "e4m3") @ mxq(f, 0, "e4m3")) / e.sum(-1, keepdims=True)

@@ -1,0 +1,274 @@
+from contextlib import ExitStack
+
+import concourse.mybir as mybir
+from concourse.masks import make_identity
+
+F32 = mybir.dt.float32
+BF16 = mybir.dt.bfloat16
+U32 = mybir.dt.uint32
+U8 = mybir.dt.uint8
+FP8X4 = mybir.dt.float8_e4m3fn_x4
+ACT = mybir.ActivationFunctionType
+ALU = mybir.AluOpType
+AXIS = mybir.AxisListType
+
+P = 128
+PACK = 4
+PASSES = 2
+SLABS = PASSES * PACK
+FRAMES = 1024
+FEATS = 1024
+BANK = 512
+HALVES = 2
+PAIR = 2
+CHUNKS = FEATS // (PAIR * P)
+EPS = 1e-6
+FLOPS = 2 * 2 * FRAMES * FRAMES * FEATS
+
+
+def tile_custommodel_pa_kernel(tc, frame_embeddings, tau_global_prime, out):
+    nc = tc.nc
+    f_rows = frame_embeddings.rearrange("(g p t) d -> p g t d", g=PASSES, t=PACK)
+    out_rows = out.rearrange("(g p t) d -> p g t d", g=PASSES, t=PACK)
+
+    with ExitStack() as stack:
+        keep = stack.enter_context(tc.tile_pool(name="keep", bufs=1))
+        work = stack.enter_context(tc.tile_pool(name="work", bufs=3))
+        results = stack.enter_context(tc.tile_pool(name="results", bufs=4))
+        psum_score = stack.enter_context(tc.psum_pool(name="psum_score", bufs=2 * HALVES))
+        stack.enter_context(tc.manual_schedule())
+
+        f_sb = keep.tile([P, SLABS, FEATS], BF16, align_bytes=64)
+        ident = keep.tile([P, P], F32)
+        nf_codes = keep.tile([P, PASSES, FRAMES], U32, align_bytes=64)
+        nf_scales = keep.tile([P, PASSES, FRAMES], U8, align_bytes=64)
+        f_codes = keep.tile([P, PASSES, FEATS], U32, align_bytes=64)
+        f_scales = keep.tile([P, PASSES, FEATS], U8, align_bytes=64)
+        sumsq = keep.tile([P, SLABS], F32)
+        half_sum = keep.tile([P, SLABS, HALVES], F32)
+        inv_tau = keep.tile([P, 1], F32)
+        norm = keep.tile([P, SLABS], F32)
+        root_of_one = keep.tile([P, 1], F32)
+        one = keep.tile([P, 1], F32)
+        norm_eps = keep.tile([P, SLABS], F32)
+        inv_norm = keep.tile([P, SLABS], F32)
+        row_sum = keep.tile([P, SLABS], F32)
+        inv_sum = keep.tile([P, SLABS], F32)
+        half_max = keep.tile([P, SLABS, HALVES], F32)
+        exp_bias = keep.tile([P, SLABS], F32)
+        score_scale = keep.tile([P, 1], F32)
+        minus_scale = keep.tile([P, 1], F32)
+        tau_sb = keep.tile([P, 1], BF16)
+
+        nc.scalar.dma_start(out=tau_sb[:], in_=tau_global_prime.partition_broadcast(P))
+        for b in range(SLABS):
+            nc.sync.dma_start(out=f_sb[:, b, :], in_=f_rows[:, b // PACK, b % PACK, :])
+        make_identity(nc, ident[:])
+        nc.vector.memset(one[:], 1.0)
+        nc.scalar.sqrt(out=root_of_one[:], in_=one[:])
+
+        def turn(pool, rows):
+            words = rows[:].bitcast(F32)
+            turned = pool.tile([P, CHUNKS, P], F32, name="turned")
+            for q in range(CHUNKS):
+                nc.tensor.transpose(turned[:, q, :], words[:, q * P : (q + 1) * P], ident[:])
+            return turned
+
+        def group(copy, turned):
+            grouped = work.tile([P, PASSES * P * PACK], BF16, name="grouped", align_bytes=64)
+            copy(
+                out=grouped[:].bitcast(F32).rearrange("k (g r u) -> k g r u", g=PASSES, u=PAIR),
+                in_=turned[:].rearrange("k (g u) r -> k g r u", u=PAIR),
+            )
+            return grouped
+
+        scores = {}
+
+        def new_score_banks(b):
+            for h in range(HALVES):
+                scores[b, h] = psum_score.tile([P, BANK], F32, name="scores")
+
+        def score_matmuls(b, h):
+            rows = slice(b * P, (b + 1) * P)
+            cols = slice(h * BANK, (h + 1) * BANK)
+            for g in range(PASSES):
+                nc.tensor.matmul_mx(
+                    out=scores[b, h][:],
+                    lhsT=nf_codes[:, g, rows].bitcast(FP8X4),
+                    lhsT_scale=nf_scales[:, g, rows],
+                    rhs=nf_codes[:, g, cols].bitcast(FP8X4),
+                    rhs_scale=nf_scales[:, g, cols],
+                    start=(g == 0),
+                    stop=(g == PASSES - 1),
+                )
+
+        def half_maximum(b, h):
+            nc.vector.reduce_max(out=half_max[:, b, h : h + 1], in_=scores[b, h][:], axis=AXIS.X)
+
+        def bias_from_maximum(b):
+            nc.vector.tensor_scalar(
+                out=exp_bias[:, b : b + 1],
+                in0=half_max[:, b, 0:1],
+                scalar1=half_max[:, b, 1:2],
+                scalar2=minus_scale[:, 0:1],
+                op0=ALU.max,
+                op1=ALU.mult,
+            )
+
+        nf_turned = {}
+        nf_grouped = {}
+        f_grouped = {}
+
+        def sum_of_squares(b):
+            squares = work.tile([P, FEATS], BF16, name="squares")
+            nc.scalar.activation(
+                out=squares[:], in_=f_sb[:, b, :], func=ACT.Square, accum_out=sumsq[:, b : b + 1]
+            )
+
+        def inverse_norms(g):
+            cols = slice(g * PACK, (g + 1) * PACK)
+            nc.scalar.sqrt(out=norm[:, cols], in_=sumsq[:, cols])
+            nc.vector.tensor_scalar_add(out=norm_eps[:, cols], in0=norm[:, cols], scalar1=EPS)
+            nc.vector.reciprocal(out=inv_norm[:, cols], in_=norm_eps[:, cols])
+
+        def normalise_and_turn(pool, b):
+            nf = work.tile([P, FEATS], BF16, name="nf")
+            nc.vector.tensor_scalar_mul(out=nf[:], in0=f_sb[:, b, :], scalar1=inv_norm[:, b : b + 1])
+            nf_turned[b] = turn(pool, nf)
+
+        def quantise_nf(b):
+            cols = slice(b * P, (b + 1) * P)
+            for g in range(PASSES):
+                nc.vector.quantize_mx(
+                    out=nf_codes[:, g, cols].bitcast(FP8X4),
+                    scales=nf_scales[:, g, cols],
+                    in_=nf_grouped[b][:, g * P * PACK : (g + 1) * P * PACK],
+                )
+
+        def regroup_f(piece):
+            g, h = divmod(piece, HALVES)
+            f_grouped[piece] = work.tile([P, BANK, PACK], BF16, name="f_grouped", align_bytes=64)
+            nc.vector.tensor_copy(
+                out=f_grouped[piece][:].rearrange("p (c i) t -> p c t i", i=4),
+                in_=f_sb[:, g * PACK : (g + 1) * PACK, h * BANK : (h + 1) * BANK].rearrange(
+                    "p t (c i) -> p c t i", i=4
+                ),
+            )
+
+        def quantise_f(piece):
+            g, h = divmod(piece, HALVES)
+            cols = slice(h * BANK, (h + 1) * BANK)
+            nc.vector.quantize_mx(
+                out=f_codes[:, g, cols].bitcast(FP8X4),
+                scales=f_scales[:, g, cols],
+                in_=f_grouped[piece][:].rearrange("p d t -> p (d t)"),
+            )
+
+        TURN_AT = PACK
+        GROUP_AT = TURN_AT + 2
+        QUANT_AT = GROUP_AT + 1
+        F_PIECES = PASSES * HALVES
+        F_FROM = 2
+        new_score_banks(0)
+        new_score_banks(1)
+        with tc.psum_pool(name="psum_nf", bufs=4) as psum_nf:
+            for step in range(SLABS + QUANT_AT):
+                if step < SLABS:
+                    sum_of_squares(step)
+                if 0 <= step - TURN_AT < SLABS:
+                    normalise_and_turn(psum_nf, step - TURN_AT)
+                if 0 <= step - GROUP_AT < SLABS:
+                    nf_grouped[step - GROUP_AT] = group(nc.scalar.copy, nf_turned[step - GROUP_AT])
+                if 0 <= step - QUANT_AT < SLABS:
+                    quantise_nf(step - QUANT_AT)
+                if 0 <= step - F_FROM < F_PIECES:
+                    regroup_f(step - F_FROM)
+                if 0 <= step - F_FROM - 1 < F_PIECES:
+                    quantise_f(step - F_FROM - 1)
+                if step < SLABS and step % PACK == PACK - 1:
+                    inverse_norms(step // PACK)
+                if step == SLABS - 1 + TURN_AT:
+                    score_matmuls(0, 0)
+                    score_matmuls(1, 0)
+                if step == SLABS + TURN_AT:
+                    half_maximum(0, 0)
+                    half_maximum(1, 0)
+
+        psum_turn = stack.enter_context(tc.psum_pool(name="psum_turn", bufs=2, reuse_waits="tile"))
+        psum_out = stack.enter_context(tc.psum_pool(name="psum_out", bufs=HALVES, reuse_waits="tile"))
+        e_rows = {}
+        e_grouped = {}
+        e_codes = {}
+        e_scales = {}
+
+        def exponentials(b):
+            e_rows[b] = work.tile([P, FRAMES], BF16, name="e_rows")
+            for g in range(HALVES):
+                nc.scalar.activation(
+                    out=e_rows[b][:, g * BANK : (g + 1) * BANK].rearrange("i (u p v) -> i u p v", u=PAIR, v=PAIR),
+                    in_=scores[b, g][:].rearrange("i (u v p) -> i u p v", u=PAIR, v=PAIR),
+                    func=ACT.Exp,
+                    bias=exp_bias[:, b : b + 1],
+                    scale=score_scale[:, 0:1],
+                    accum_out=half_sum[:, b, g : g + 1],
+                )
+
+        def quantise_e(b):
+            e_codes[b] = work.tile([P, PASSES, P], U32, name="e_codes", align_bytes=64)
+            e_scales[b] = work.tile([P, PASSES, P], U8, name="e_scales", align_bytes=64)
+            nc.vector.quantize_mx(
+                out=e_codes[b][:].rearrange("p g i -> p (g i)").bitcast(FP8X4),
+                scales=e_scales[b][:].rearrange("p g i -> p (g i)"),
+                in_=e_grouped[b][:],
+            )
+
+        def weighted_sum(b):
+            for h in range(HALVES):
+                cols = slice(h * BANK, (h + 1) * BANK)
+                acc = psum_out.tile([P, BANK], F32, name="acc")
+                for g in range(PASSES):
+                    nc.tensor.matmul_mx(
+                        out=acc[:],
+                        lhsT=e_codes[b][:, g, :].bitcast(FP8X4),
+                        lhsT_scale=e_scales[b][:, g, :],
+                        rhs=f_codes[:, g, cols].bitcast(FP8X4),
+                        rhs_scale=f_scales[:, g, cols],
+                        start=(g == 0),
+                        stop=(g == PASSES - 1),
+                    )
+                result = results.tile([P, BANK], F32, name="result")
+                if h == 1 and b % 2 == 1:
+                    nc.vector.tensor_scalar_mul(out=result[:], in0=acc[:], scalar1=inv_sum[:, b : b + 1])
+                else:
+                    nc.scalar.activation(out=result[:], in_=acc[:], func=ACT.Copy, scale=inv_sum[:, b : b + 1])
+                nc.sync.dma_start(out=out_rows[:, b // PACK, b % PACK, cols], in_=result[:])
+
+        nc.scalar.activation(out=inv_tau[:], in_=tau_sb[:], func=ACT.Exp, scale=-1.0)
+        nc.vector.tensor_scalar_mul(out=score_scale[:], in0=inv_tau[:], scalar1=1.0 / 32.0)
+        nc.vector.tensor_scalar_mul(out=minus_scale[:], in0=inv_tau[:], scalar1=-1.0 / 32.0)
+        for b in range(2):
+            score_matmuls(b, 1)
+        for b in range(2):
+            half_maximum(b, 1)
+            bias_from_maximum(b)
+        exponentials(0)
+        for b in range(SLABS + 1):
+            ahead = b + 2
+            if b < SLABS:
+                e_grouped[b] = group(nc.vector.tensor_copy, turn(psum_turn, e_rows[b]))
+                nc.vector.tensor_add(out=row_sum[:, b : b + 1], in0=half_sum[:, b, 0:1], in1=half_sum[:, b, 1:2])
+            if ahead < SLABS:
+                new_score_banks(ahead)
+                score_matmuls(ahead, 0)
+                score_matmuls(ahead, 1)
+                half_maximum(ahead, 0)
+            if b < SLABS:
+                nc.vector.reciprocal(out=inv_sum[:, b : b + 1], in_=row_sum[:, b : b + 1])
+                quantise_e(b)
+            if ahead < SLABS:
+                half_maximum(ahead, 1)
+                bias_from_maximum(ahead)
+            if b + 1 < SLABS:
+                exponentials(b + 1)
+            if b >= 1:
+                weighted_sum(b - 1)

@@ -23,6 +23,10 @@ HALVES = 2
 PAIR = 2
 CHUNKS = FEATS // (PAIR * P)
 EPS = 1e-6
+DUO = 2
+DUOS = SLABS // DUO
+VECTOR_SQUARES = (1,)
+AHEAD = 3
 FLOPS = 2 * 2 * FRAMES * FRAMES * FEATS
 
 
@@ -35,7 +39,7 @@ def tile_custommodel_pa_kernel(tc, frame_embeddings, tau_global_prime, out):
         keep = stack.enter_context(tc.tile_pool(name="keep", bufs=1))
         work = stack.enter_context(tc.tile_pool(name="work", bufs=3))
         results = stack.enter_context(tc.tile_pool(name="results", bufs=4))
-        psum_score = stack.enter_context(tc.psum_pool(name="psum_score", bufs=2 * HALVES))
+        psum_first = stack.enter_context(tc.psum_pool(name="psum_first", bufs=AHEAD))
         stack.enter_context(tc.manual_schedule())
 
         f_sb = keep.tile([P, SLABS, FEATS], BF16, align_bytes=64)
@@ -44,15 +48,17 @@ def tile_custommodel_pa_kernel(tc, frame_embeddings, tau_global_prime, out):
         nf_scales = keep.tile([P, PASSES, FRAMES], U8, align_bytes=64)
         f_codes = keep.tile([P, PASSES, FEATS], U32, align_bytes=64)
         f_scales = keep.tile([P, PASSES, FEATS], U8, align_bytes=64)
-        sumsq = keep.tile([P, SLABS], F32)
+        sumsq = []
+        for duo in range(DUOS):
+            sumsq.append(keep.tile([P, DUO], F32, name="sumsq%d" % duo))
         half_sum = keep.tile([P, SLABS, HALVES], F32)
+        row_sum = keep.tile([P, SLABS], F32)
         inv_tau = keep.tile([P, 1], F32)
         norm = keep.tile([P, SLABS], F32)
         root_of_one = keep.tile([P, 1], F32)
         one = keep.tile([P, 1], F32)
         norm_eps = keep.tile([P, SLABS], F32)
         inv_norm = keep.tile([P, SLABS], F32)
-        row_sum = keep.tile([P, SLABS], F32)
         inv_sum = keep.tile([P, SLABS], F32)
         half_max = keep.tile([P, SLABS, HALVES], F32)
         exp_bias = keep.tile([P, SLABS], F32)
@@ -60,9 +66,9 @@ def tile_custommodel_pa_kernel(tc, frame_embeddings, tau_global_prime, out):
         minus_scale = keep.tile([P, 1], F32)
         tau_sb = keep.tile([P, 1], BF16)
 
-        nc.scalar.dma_start(out=tau_sb[:], in_=tau_global_prime.partition_broadcast(P))
         for b in range(SLABS):
             nc.sync.dma_start(out=f_sb[:, b, :], in_=f_rows[:, b // PACK, b % PACK, :])
+        nc.sync.dma_start(out=tau_sb[:], in_=tau_global_prime.partition_broadcast(P))
         make_identity(nc, ident[:])
         nc.vector.memset(one[:], 1.0)
         nc.scalar.sqrt(out=root_of_one[:], in_=one[:])
@@ -74,21 +80,13 @@ def tile_custommodel_pa_kernel(tc, frame_embeddings, tau_global_prime, out):
                 nc.tensor.transpose(turned[:, q, :], words[:, q * P : (q + 1) * P], ident[:])
             return turned
 
-        def group(copy, turned):
-            grouped = work.tile([P, PASSES * P * PACK], BF16, name="grouped", align_bytes=64)
-            copy(
-                out=grouped[:].bitcast(F32).rearrange("k (g r u) -> k g r u", g=PASSES, u=PAIR),
-                in_=turned[:].rearrange("k (g u) r -> k g r u", u=PAIR),
-            )
-            return grouped
-
         scores = {}
 
-        def new_score_banks(b):
-            for h in range(HALVES):
-                scores[b, h] = psum_score.tile([P, BANK], F32, name="scores")
-
         def score_matmuls(b, h):
+            if h == 0:
+                scores[b, h] = psum_first.tile([P, BANK], F32, name="first_scores")
+            else:
+                scores[b, h] = psum_second.tile([P, BANK], F32, name="second_scores")
             rows = slice(b * P, (b + 1) * P)
             cols = slice(h * BANK, (h + 1) * BANK)
             for g in range(PASSES):
@@ -120,14 +118,28 @@ def tile_custommodel_pa_kernel(tc, frame_embeddings, tau_global_prime, out):
         f_grouped = {}
 
         def sum_of_squares(b):
-            squares = work.tile([P, FEATS], BF16, name="squares")
-            nc.scalar.activation(
-                out=squares[:], in_=f_sb[:, b, :], func=ACT.Square, accum_out=sumsq[:, b : b + 1]
-            )
+            total = sumsq[b // DUO][:, b % DUO : b % DUO + 1]
+            if b in VECTOR_SQUARES:
+                squares = work.tile([P, FEATS], BF16, name="vector_squares")
+                nc.vector.scalar_tensor_tensor(
+                    out=squares[:],
+                    in0=f_sb[:, b, :],
+                    scalar=1.0,
+                    in1=f_sb[:, b, :],
+                    op0=ALU.mult,
+                    op1=ALU.mult,
+                    accum_out=total,
+                )
+            else:
+                squares = work.tile([P, FEATS], BF16, name="scalar_squares")
+                nc.scalar.activation(out=squares[:], in_=f_sb[:, b, :], func=ACT.Square, accum_out=total)
 
-        def inverse_norms(g):
-            cols = slice(g * PACK, (g + 1) * PACK)
-            nc.scalar.sqrt(out=norm[:, cols], in_=sumsq[:, cols])
+        def roots(duo):
+            cols = slice(duo * DUO, (duo + 1) * DUO)
+            nc.scalar.sqrt(out=norm[:, cols], in_=sumsq[duo][:])
+
+        def inverse_norms(duo):
+            cols = slice(duo * DUO, (duo + 1) * DUO)
             nc.vector.tensor_scalar_add(out=norm_eps[:, cols], in0=norm[:, cols], scalar1=EPS)
             nc.vector.reciprocal(out=inv_norm[:, cols], in_=norm_eps[:, cols])
 
@@ -136,13 +148,23 @@ def tile_custommodel_pa_kernel(tc, frame_embeddings, tau_global_prime, out):
             nc.vector.tensor_scalar_mul(out=nf[:], in0=f_sb[:, b, :], scalar1=inv_norm[:, b : b + 1])
             nf_turned[b] = turn(pool, nf)
 
-        def quantise_nf(b):
-            cols = slice(b * P, (b + 1) * P)
+        def group_nf(b, copy):
+            duo, member = divmod(b, DUO)
+            if member == 0:
+                nf_grouped[duo] = work.tile([P, PASSES, DUO * P * PACK], BF16, name="nf_grouped", align_bytes=64)
+            cols = slice(member * P * PACK, (member + 1) * P * PACK)
+            copy(
+                out=nf_grouped[duo][:, :, cols].bitcast(F32).rearrange("k g (r u) -> k g r u", u=PAIR),
+                in_=nf_turned[b][:].rearrange("k (g u) r -> k g r u", u=PAIR),
+            )
+
+        def quantise_nf(duo):
+            cols = slice(duo * DUO * P, (duo + 1) * DUO * P)
             for g in range(PASSES):
                 nc.vector.quantize_mx(
                     out=nf_codes[:, g, cols].bitcast(FP8X4),
                     scales=nf_scales[:, g, cols],
-                    in_=nf_grouped[b][:, g * P * PACK : (g + 1) * P * PACK],
+                    in_=nf_grouped[duo][:, g, :],
                 )
 
         def regroup_f(piece):
@@ -164,39 +186,64 @@ def tile_custommodel_pa_kernel(tc, frame_embeddings, tau_global_prime, out):
                 in_=f_grouped[piece][:].rearrange("p d t -> p (d t)"),
             )
 
-        TURN_AT = PACK
-        GROUP_AT = TURN_AT + 2
-        QUANT_AT = GROUP_AT + 1
-        F_PIECES = PASSES * HALVES
-        F_FROM = 2
-        new_score_banks(0)
-        new_score_banks(1)
-        with tc.psum_pool(name="psum_nf", bufs=4) as psum_nf:
-            for step in range(SLABS + QUANT_AT):
-                if step < SLABS:
-                    sum_of_squares(step)
-                if 0 <= step - TURN_AT < SLABS:
-                    normalise_and_turn(psum_nf, step - TURN_AT)
-                if 0 <= step - GROUP_AT < SLABS:
-                    nf_grouped[step - GROUP_AT] = group(nc.scalar.copy, nf_turned[step - GROUP_AT])
-                if 0 <= step - QUANT_AT < SLABS:
-                    quantise_nf(step - QUANT_AT)
-                if 0 <= step - F_FROM < F_PIECES:
-                    regroup_f(step - F_FROM)
-                if 0 <= step - F_FROM - 1 < F_PIECES:
-                    quantise_f(step - F_FROM - 1)
-                if step < SLABS and step % PACK == PACK - 1:
-                    inverse_norms(step // PACK)
-                if step == SLABS - 1 + TURN_AT:
-                    score_matmuls(0, 0)
-                    score_matmuls(1, 0)
-                if step == SLABS + TURN_AT:
-                    half_maximum(0, 0)
-                    half_maximum(1, 0)
+        def temperature_table():
+            nc.scalar.activation(out=inv_tau[:], in_=tau_sb[:], func=ACT.Exp, scale=-1.0)
 
-        psum_turn = stack.enter_context(tc.psum_pool(name="psum_turn", bufs=2, reuse_waits="tile"))
-        psum_out = stack.enter_context(tc.psum_pool(name="psum_out", bufs=HALVES, reuse_waits="tile"))
+        def temperature():
+            nc.vector.tensor_scalar_mul(out=score_scale[:], in0=inv_tau[:], scalar1=1.0 / 32.0)
+            nc.vector.tensor_scalar_mul(out=minus_scale[:], in0=inv_tau[:], scalar1=-1.0 / 32.0)
+
+        with tc.psum_pool(name="psum_nf", bufs=4) as psum_nf:
+            sum_of_squares(0)
+            sum_of_squares(1)
+            roots(0)
+            inverse_norms(0)
+            normalise_and_turn(psum_nf, 0)
+            normalise_and_turn(psum_nf, 1)
+            regroup_f(0)
+            sum_of_squares(2)
+            sum_of_squares(3)
+            roots(1)
+            inverse_norms(1)
+            normalise_and_turn(psum_nf, 2)
+            normalise_and_turn(psum_nf, 3)
+            group_nf(0, nc.scalar.copy)
+            group_nf(1, nc.scalar.copy)
+            quantise_f(0)
+            quantise_nf(0)
+            regroup_f(1)
+            sum_of_squares(4)
+            sum_of_squares(5)
+            roots(2)
+            inverse_norms(2)
+            normalise_and_turn(psum_nf, 4)
+            normalise_and_turn(psum_nf, 5)
+            group_nf(2, nc.scalar.copy)
+            group_nf(3, nc.scalar.copy)
+            quantise_f(1)
+            quantise_nf(1)
+            regroup_f(2)
+            sum_of_squares(6)
+            sum_of_squares(7)
+            roots(3)
+            inverse_norms(3)
+            normalise_and_turn(psum_nf, 6)
+            normalise_and_turn(psum_nf, 7)
+            group_nf(4, nc.scalar.copy)
+            group_nf(5, nc.scalar.copy)
+            quantise_f(2)
+            quantise_nf(2)
+            score_matmuls(0, 0)
+            score_matmuls(1, 0)
+            score_matmuls(2, 0)
+            group_nf(6, nc.scalar.copy)
+            group_nf(7, nc.scalar.copy)
+
+        psum_second = stack.enter_context(tc.psum_pool(name="psum_second", bufs=2, reuse_waits="tile"))
+        psum_turn = stack.enter_context(tc.psum_pool(name="psum_turn", bufs=1, reuse_waits="tile"))
+        psum_out = stack.enter_context(tc.psum_pool(name="psum_out", bufs=2, reuse_waits="tile"))
         e_rows = {}
+        e_turned = {}
         e_grouped = {}
         e_codes = {}
         e_scales = {}
@@ -213,6 +260,24 @@ def tile_custommodel_pa_kernel(tc, frame_embeddings, tau_global_prime, out):
                     accum_out=half_sum[:, b, g : g + 1],
                 )
 
+        def sum_halves(b):
+            nc.scalar.activation(
+                out=row_sum[:, b : b + 1], in_=half_sum[:, b, 0:1], func=ACT.Identity, bias=half_sum[:, b, 1:2]
+            )
+
+        def inverse_sum(b):
+            nc.vector.reciprocal(out=inv_sum[:, b : b + 1], in_=row_sum[:, b : b + 1])
+
+        def turn_e(b):
+            e_turned[b] = turn(psum_turn, e_rows[b])
+
+        def group_e(b):
+            e_grouped[b] = work.tile([P, PASSES * P * PACK], BF16, name="e_grouped", align_bytes=64)
+            nc.vector.tensor_copy(
+                out=e_grouped[b][:].bitcast(F32).rearrange("k (g r u) -> k g r u", g=PASSES, u=PAIR),
+                in_=e_turned[b][:].rearrange("k (g u) r -> k g r u", u=PAIR),
+            )
+
         def quantise_e(b):
             e_codes[b] = work.tile([P, PASSES, P], U32, name="e_codes", align_bytes=64)
             e_scales[b] = work.tile([P, PASSES, P], U8, name="e_scales", align_bytes=64)
@@ -222,53 +287,150 @@ def tile_custommodel_pa_kernel(tc, frame_embeddings, tau_global_prime, out):
                 in_=e_grouped[b][:],
             )
 
-        def weighted_sum(b):
-            for h in range(HALVES):
-                cols = slice(h * BANK, (h + 1) * BANK)
-                acc = psum_out.tile([P, BANK], F32, name="acc")
-                for g in range(PASSES):
-                    nc.tensor.matmul_mx(
-                        out=acc[:],
-                        lhsT=e_codes[b][:, g, :].bitcast(FP8X4),
-                        lhsT_scale=e_scales[b][:, g, :],
-                        rhs=f_codes[:, g, cols].bitcast(FP8X4),
-                        rhs_scale=f_scales[:, g, cols],
-                        start=(g == 0),
-                        stop=(g == PASSES - 1),
-                    )
-                result = results.tile([P, BANK], F32, name="result")
-                if h == 1 and b % 2 == 1:
-                    nc.vector.tensor_scalar_mul(out=result[:], in0=acc[:], scalar1=inv_sum[:, b : b + 1])
-                else:
-                    nc.scalar.activation(out=result[:], in_=acc[:], func=ACT.Copy, scale=inv_sum[:, b : b + 1])
-                nc.sync.dma_start(out=out_rows[:, b // PACK, b % PACK, cols], in_=result[:])
+        acc = {}
 
-        nc.scalar.activation(out=inv_tau[:], in_=tau_sb[:], func=ACT.Exp, scale=-1.0)
-        nc.vector.tensor_scalar_mul(out=score_scale[:], in0=inv_tau[:], scalar1=1.0 / 32.0)
-        nc.vector.tensor_scalar_mul(out=minus_scale[:], in0=inv_tau[:], scalar1=-1.0 / 32.0)
-        for b in range(2):
-            score_matmuls(b, 1)
-        for b in range(2):
-            half_maximum(b, 1)
-            bias_from_maximum(b)
+        def weighted_sum(b, h):
+            cols = slice(h * BANK, (h + 1) * BANK)
+            acc[b, h] = psum_out.tile([P, BANK], F32, name="acc")
+            for g in range(PASSES):
+                nc.tensor.matmul_mx(
+                    out=acc[b, h][:],
+                    lhsT=e_codes[b][:, g, :].bitcast(FP8X4),
+                    lhsT_scale=e_scales[b][:, g, :],
+                    rhs=f_codes[:, g, cols].bitcast(FP8X4),
+                    rhs_scale=f_scales[:, g, cols],
+                    start=(g == 0),
+                    stop=(g == PASSES - 1),
+                )
+
+        def divide_and_store(b, h, on_vector):
+            cols = slice(h * BANK, (h + 1) * BANK)
+            result = results.tile([P, BANK], F32, name="result")
+            if on_vector:
+                nc.vector.tensor_scalar_mul(out=result[:], in0=acc[b, h][:], scalar1=inv_sum[:, b : b + 1])
+            else:
+                nc.scalar.activation(out=result[:], in_=acc[b, h][:], func=ACT.Copy, scale=inv_sum[:, b : b + 1])
+            nc.sync.dma_start(out=out_rows[:, b // PACK, b % PACK, cols], in_=result[:])
+
+        half_maximum(0, 0)
+        half_maximum(1, 0)
+        quantise_nf(3)
+        temperature_table()
+        score_matmuls(0, 1)
+        score_matmuls(1, 1)
+        temperature()
+        half_maximum(0, 1)
+        bias_from_maximum(0)
+        half_maximum(1, 1)
+        bias_from_maximum(1)
+        regroup_f(3)
+        half_maximum(2, 0)
+        quantise_f(3)
         exponentials(0)
-        for b in range(SLABS + 1):
-            ahead = b + 2
-            if b < SLABS:
-                e_grouped[b] = group(nc.vector.tensor_copy, turn(psum_turn, e_rows[b]))
-                nc.vector.tensor_add(out=row_sum[:, b : b + 1], in0=half_sum[:, b, 0:1], in1=half_sum[:, b, 1:2])
-            if ahead < SLABS:
-                new_score_banks(ahead)
-                score_matmuls(ahead, 0)
-                score_matmuls(ahead, 1)
-                half_maximum(ahead, 0)
-            if b < SLABS:
-                nc.vector.reciprocal(out=inv_sum[:, b : b + 1], in_=row_sum[:, b : b + 1])
-                quantise_e(b)
-            if ahead < SLABS:
-                half_maximum(ahead, 1)
-                bias_from_maximum(ahead)
-            if b + 1 < SLABS:
-                exponentials(b + 1)
-            if b >= 1:
-                weighted_sum(b - 1)
+        sum_halves(0)
+        turn_e(0)
+        group_e(0)
+        score_matmuls(2, 1)
+        score_matmuls(3, 0)
+        half_maximum(2, 1)
+        bias_from_maximum(2)
+        inverse_sum(0)
+        quantise_e(0)
+        half_maximum(3, 0)
+        exponentials(1)
+        sum_halves(1)
+        turn_e(1)
+        group_e(1)
+        score_matmuls(3, 1)
+        score_matmuls(4, 0)
+        half_maximum(3, 1)
+        bias_from_maximum(3)
+        inverse_sum(1)
+        quantise_e(1)
+        half_maximum(4, 0)
+        exponentials(2)
+        weighted_sum(0, 0)
+        weighted_sum(0, 1)
+        divide_and_store(0, 0, False)
+        divide_and_store(0, 1, False)
+        sum_halves(2)
+        turn_e(2)
+        group_e(2)
+        score_matmuls(4, 1)
+        score_matmuls(5, 0)
+        half_maximum(4, 1)
+        bias_from_maximum(4)
+        inverse_sum(2)
+        quantise_e(2)
+        half_maximum(5, 0)
+        exponentials(3)
+        weighted_sum(1, 0)
+        weighted_sum(1, 1)
+        divide_and_store(1, 0, False)
+        divide_and_store(1, 1, False)
+        sum_halves(3)
+        turn_e(3)
+        group_e(3)
+        score_matmuls(5, 1)
+        score_matmuls(6, 0)
+        half_maximum(5, 1)
+        bias_from_maximum(5)
+        inverse_sum(3)
+        quantise_e(3)
+        half_maximum(6, 0)
+        exponentials(4)
+        weighted_sum(2, 0)
+        weighted_sum(2, 1)
+        divide_and_store(2, 0, False)
+        divide_and_store(2, 1, False)
+        sum_halves(4)
+        turn_e(4)
+        group_e(4)
+        score_matmuls(6, 1)
+        score_matmuls(7, 0)
+        half_maximum(6, 1)
+        bias_from_maximum(6)
+        inverse_sum(4)
+        quantise_e(4)
+        half_maximum(7, 0)
+        exponentials(5)
+        weighted_sum(3, 0)
+        weighted_sum(3, 1)
+        divide_and_store(3, 0, False)
+        divide_and_store(3, 1, False)
+        sum_halves(5)
+        turn_e(5)
+        group_e(5)
+        score_matmuls(7, 1)
+        half_maximum(7, 1)
+        bias_from_maximum(7)
+        inverse_sum(5)
+        quantise_e(5)
+        exponentials(6)
+        weighted_sum(4, 0)
+        weighted_sum(4, 1)
+        divide_and_store(4, 0, False)
+        divide_and_store(4, 1, False)
+        sum_halves(6)
+        turn_e(6)
+        group_e(6)
+        inverse_sum(6)
+        quantise_e(6)
+        exponentials(7)
+        weighted_sum(5, 0)
+        weighted_sum(5, 1)
+        divide_and_store(5, 0, False)
+        divide_and_store(5, 1, False)
+        sum_halves(7)
+        turn_e(7)
+        group_e(7)
+        inverse_sum(7)
+        quantise_e(7)
+        weighted_sum(6, 0)
+        weighted_sum(6, 1)
+        divide_and_store(6, 0, False)
+        divide_and_store(6, 1, False)
+        weighted_sum(7, 0)
+        weighted_sum(7, 1)
+        divide_and_store(7, 0, False)
+        divide_and_store(7, 1, True)

@@ -26,7 +26,9 @@ EPS = 1e-6
 DUO = 2
 DUOS = SLABS // DUO
 VECTOR_SQUARES = (1,)
-AHEAD = 3
+NF_BANKS = (4, 5, 6, 7)
+TURN_BANKS = (7,)
+OUT_BANKS = (3, 6)
 FLOPS = 2 * 2 * FRAMES * FRAMES * FEATS
 
 
@@ -38,8 +40,12 @@ def tile_custommodel_pa_kernel(tc, frame_embeddings, tau_global_prime, out):
     with ExitStack() as stack:
         keep = stack.enter_context(tc.tile_pool(name="keep", bufs=1))
         work = stack.enter_context(tc.tile_pool(name="work", bufs=3))
-        results = stack.enter_context(tc.tile_pool(name="results", bufs=4))
-        psum_first = stack.enter_context(tc.psum_pool(name="psum_first", bufs=AHEAD))
+        results = stack.enter_context(tc.tile_pool(name="results", bufs=8))
+        psum = stack.enter_context(tc.psum_pool(name="psum", bufs=1, reuse_waits="tile"))
+
+        def bank(number, shape):
+            return psum.tile(shape, F32, name="bank%d" % number)
+
         stack.enter_context(tc.manual_schedule())
 
         f_sb = keep.tile([P, SLABS, FEATS], BF16, align_bytes=64)
@@ -73,20 +79,22 @@ def tile_custommodel_pa_kernel(tc, frame_embeddings, tau_global_prime, out):
         nc.vector.memset(one[:], 1.0)
         nc.scalar.sqrt(out=root_of_one[:], in_=one[:])
 
-        def turn(pool, rows):
+        def turn(number, rows):
             words = rows[:].bitcast(F32)
-            turned = pool.tile([P, CHUNKS, P], F32, name="turned")
+            turned = bank(number, [P, CHUNKS, P])
             for q in range(CHUNKS):
                 nc.tensor.transpose(turned[:, q, :], words[:, q * P : (q + 1) * P], ident[:])
             return turned
 
         scores = {}
 
-        def score_matmuls(b, h):
+        def score_bank(b, h):
             if h == 0:
-                scores[b, h] = psum_first.tile([P, BANK], F32, name="first_scores")
-            else:
-                scores[b, h] = psum_second.tile([P, BANK], F32, name="second_scores")
+                return b % 3
+            return 6 if b == 2 else 4 + (b + b // 3) % 2
+
+        def score_matmuls(b, h):
+            scores[b, h] = bank(score_bank(b, h), [P, BANK])
             rows = slice(b * P, (b + 1) * P)
             cols = slice(h * BANK, (h + 1) * BANK)
             for g in range(PASSES):
@@ -143,10 +151,10 @@ def tile_custommodel_pa_kernel(tc, frame_embeddings, tau_global_prime, out):
             nc.vector.tensor_scalar_add(out=norm_eps[:, cols], in0=norm[:, cols], scalar1=EPS)
             nc.vector.reciprocal(out=inv_norm[:, cols], in_=norm_eps[:, cols])
 
-        def normalise_and_turn(pool, b):
+        def normalise_and_turn(b):
             nf = work.tile([P, FEATS], BF16, name="nf")
             nc.vector.tensor_scalar_mul(out=nf[:], in0=f_sb[:, b, :], scalar1=inv_norm[:, b : b + 1])
-            nf_turned[b] = turn(pool, nf)
+            nf_turned[b] = turn(NF_BANKS[b % len(NF_BANKS)], nf)
 
         def group_nf(b, copy):
             duo, member = divmod(b, DUO)
@@ -167,12 +175,13 @@ def tile_custommodel_pa_kernel(tc, frame_embeddings, tau_global_prime, out):
                     in_=nf_grouped[duo][:, g, :],
                 )
 
-        def regroup_f(piece):
+        def regroup_f(piece, copy, first, last):
             g, h = divmod(piece, HALVES)
-            f_grouped[piece] = work.tile([P, BANK, PACK], BF16, name="f_grouped", align_bytes=64)
-            nc.vector.tensor_copy(
-                out=f_grouped[piece][:].rearrange("p (c i) t -> p c t i", i=4),
-                in_=f_sb[:, g * PACK : (g + 1) * PACK, h * BANK : (h + 1) * BANK].rearrange(
+            if first == 0:
+                f_grouped[piece] = work.tile([P, BANK, PACK], BF16, name="f_grouped", align_bytes=64)
+            copy(
+                out=f_grouped[piece][:, first:last, :].rearrange("p (c i) t -> p c t i", i=4),
+                in_=f_sb[:, g * PACK : (g + 1) * PACK, h * BANK + first : h * BANK + last].rearrange(
                     "p t (c i) -> p c t i", i=4
                 ),
             )
@@ -193,55 +202,50 @@ def tile_custommodel_pa_kernel(tc, frame_embeddings, tau_global_prime, out):
             nc.vector.tensor_scalar_mul(out=score_scale[:], in0=inv_tau[:], scalar1=1.0 / 32.0)
             nc.vector.tensor_scalar_mul(out=minus_scale[:], in0=inv_tau[:], scalar1=-1.0 / 32.0)
 
-        with tc.psum_pool(name="psum_nf", bufs=4) as psum_nf:
-            sum_of_squares(0)
-            sum_of_squares(1)
-            roots(0)
-            inverse_norms(0)
-            normalise_and_turn(psum_nf, 0)
-            normalise_and_turn(psum_nf, 1)
-            regroup_f(0)
-            sum_of_squares(2)
-            sum_of_squares(3)
-            roots(1)
-            inverse_norms(1)
-            normalise_and_turn(psum_nf, 2)
-            normalise_and_turn(psum_nf, 3)
-            group_nf(0, nc.scalar.copy)
-            group_nf(1, nc.scalar.copy)
-            quantise_f(0)
-            quantise_nf(0)
-            regroup_f(1)
-            sum_of_squares(4)
-            sum_of_squares(5)
-            roots(2)
-            inverse_norms(2)
-            normalise_and_turn(psum_nf, 4)
-            normalise_and_turn(psum_nf, 5)
-            group_nf(2, nc.scalar.copy)
-            group_nf(3, nc.scalar.copy)
-            quantise_f(1)
-            quantise_nf(1)
-            regroup_f(2)
-            sum_of_squares(6)
-            sum_of_squares(7)
-            roots(3)
-            inverse_norms(3)
-            normalise_and_turn(psum_nf, 6)
-            normalise_and_turn(psum_nf, 7)
-            group_nf(4, nc.scalar.copy)
-            group_nf(5, nc.scalar.copy)
-            quantise_f(2)
-            quantise_nf(2)
-            score_matmuls(0, 0)
-            score_matmuls(1, 0)
-            score_matmuls(2, 0)
-            group_nf(6, nc.scalar.copy)
-            group_nf(7, nc.scalar.copy)
+        sum_of_squares(0)
+        sum_of_squares(1)
+        sum_of_squares(2)
+        roots(0)
+        regroup_f(0, nc.vector.tensor_copy, 0, BANK)
+        inverse_norms(0)
+        normalise_and_turn(0)
+        normalise_and_turn(1)
+        sum_of_squares(3)
+        roots(1)
+        inverse_norms(1)
+        normalise_and_turn(2)
+        normalise_and_turn(3)
+        sum_of_squares(4)
+        sum_of_squares(5)
+        roots(2)
+        quantise_f(0)
+        group_nf(0, nc.scalar.copy)
+        group_nf(1, nc.scalar.copy)
+        regroup_f(1, nc.vector.tensor_copy, 0, BANK)
+        inverse_norms(2)
+        normalise_and_turn(4)
+        normalise_and_turn(5)
+        quantise_nf(0)
+        quantise_f(1)
+        sum_of_squares(6)
+        sum_of_squares(7)
+        regroup_f(2, nc.vector.tensor_copy, 0, BANK)
+        roots(3)
+        inverse_norms(3)
+        group_nf(2, nc.scalar.copy)
+        normalise_and_turn(6)
+        group_nf(3, nc.scalar.copy)
+        normalise_and_turn(7)
+        quantise_nf(1)
+        group_nf(4, nc.scalar.copy)
+        group_nf(5, nc.scalar.copy)
+        score_matmuls(0, 0)
+        score_matmuls(1, 0)
+        score_matmuls(2, 0)
+        quantise_nf(2)
+        group_nf(6, nc.scalar.copy)
+        group_nf(7, nc.scalar.copy)
 
-        psum_second = stack.enter_context(tc.psum_pool(name="psum_second", bufs=2, reuse_waits="tile"))
-        psum_turn = stack.enter_context(tc.psum_pool(name="psum_turn", bufs=1, reuse_waits="tile"))
-        psum_out = stack.enter_context(tc.psum_pool(name="psum_out", bufs=2, reuse_waits="tile"))
         e_rows = {}
         e_turned = {}
         e_grouped = {}
@@ -269,11 +273,11 @@ def tile_custommodel_pa_kernel(tc, frame_embeddings, tau_global_prime, out):
             nc.vector.reciprocal(out=inv_sum[:, b : b + 1], in_=row_sum[:, b : b + 1])
 
         def turn_e(b):
-            e_turned[b] = turn(psum_turn, e_rows[b])
+            e_turned[b] = turn(TURN_BANKS[b % len(TURN_BANKS)], e_rows[b])
 
-        def group_e(b):
+        def group_e(b, copy):
             e_grouped[b] = work.tile([P, PASSES * P * PACK], BF16, name="e_grouped", align_bytes=64)
-            nc.vector.tensor_copy(
+            copy(
                 out=e_grouped[b][:].bitcast(F32).rearrange("k (g r u) -> k g r u", g=PASSES, u=PAIR),
                 in_=e_turned[b][:].rearrange("k (g u) r -> k g r u", u=PAIR),
             )
@@ -291,7 +295,7 @@ def tile_custommodel_pa_kernel(tc, frame_embeddings, tau_global_prime, out):
 
         def weighted_sum(b, h):
             cols = slice(h * BANK, (h + 1) * BANK)
-            acc[b, h] = psum_out.tile([P, BANK], F32, name="acc")
+            acc[b, h] = bank(OUT_BANKS[h], [P, BANK])
             for g in range(PASSES):
                 nc.tensor.matmul_mx(
                     out=acc[b, h][:],
@@ -312,56 +316,58 @@ def tile_custommodel_pa_kernel(tc, frame_embeddings, tau_global_prime, out):
                 nc.scalar.activation(out=result[:], in_=acc[b, h][:], func=ACT.Copy, scale=inv_sum[:, b : b + 1])
             nc.sync.dma_start(out=out_rows[:, b // PACK, b % PACK, cols], in_=result[:])
 
-        half_maximum(0, 0)
-        half_maximum(1, 0)
         quantise_nf(3)
+        half_maximum(0, 0)
         temperature_table()
+        regroup_f(3, nc.scalar.copy, 0, BANK // 2)
         score_matmuls(0, 1)
         score_matmuls(1, 1)
+        score_matmuls(2, 1)
         temperature()
         half_maximum(0, 1)
         bias_from_maximum(0)
+        half_maximum(1, 0)
         half_maximum(1, 1)
         bias_from_maximum(1)
-        regroup_f(3)
-        half_maximum(2, 0)
-        quantise_f(3)
         exponentials(0)
         sum_halves(0)
+        exponentials(1)
         turn_e(0)
-        group_e(0)
-        score_matmuls(2, 1)
         score_matmuls(3, 0)
+        score_matmuls(3, 1)
+        quantise_f(2)
+        group_e(0, nc.scalar.copy)
+        half_maximum(2, 0)
         half_maximum(2, 1)
         bias_from_maximum(2)
-        inverse_sum(0)
+        regroup_f(3, nc.vector.tensor_copy, BANK // 2, BANK)
         quantise_e(0)
-        half_maximum(3, 0)
-        exponentials(1)
+        quantise_f(3)
         sum_halves(1)
+        exponentials(2)
         turn_e(1)
-        group_e(1)
-        score_matmuls(3, 1)
+        group_e(1, nc.scalar.copy)
+        quantise_e(1)
+        inverse_sum(0)
+        half_maximum(3, 0)
         score_matmuls(4, 0)
         half_maximum(3, 1)
         bias_from_maximum(3)
         inverse_sum(1)
-        quantise_e(1)
         half_maximum(4, 0)
-        exponentials(2)
         weighted_sum(0, 0)
         weighted_sum(0, 1)
         divide_and_store(0, 0, False)
         divide_and_store(0, 1, False)
         sum_halves(2)
         turn_e(2)
-        group_e(2)
+        group_e(2, nc.vector.tensor_copy)
         score_matmuls(4, 1)
         score_matmuls(5, 0)
         half_maximum(4, 1)
         bias_from_maximum(4)
-        inverse_sum(2)
         quantise_e(2)
+        inverse_sum(2)
         half_maximum(5, 0)
         exponentials(3)
         weighted_sum(1, 0)
@@ -370,13 +376,13 @@ def tile_custommodel_pa_kernel(tc, frame_embeddings, tau_global_prime, out):
         divide_and_store(1, 1, False)
         sum_halves(3)
         turn_e(3)
-        group_e(3)
+        group_e(3, nc.vector.tensor_copy)
         score_matmuls(5, 1)
         score_matmuls(6, 0)
         half_maximum(5, 1)
         bias_from_maximum(5)
-        inverse_sum(3)
         quantise_e(3)
+        inverse_sum(3)
         half_maximum(6, 0)
         exponentials(4)
         weighted_sum(2, 0)
@@ -385,13 +391,13 @@ def tile_custommodel_pa_kernel(tc, frame_embeddings, tau_global_prime, out):
         divide_and_store(2, 1, False)
         sum_halves(4)
         turn_e(4)
-        group_e(4)
+        group_e(4, nc.vector.tensor_copy)
         score_matmuls(6, 1)
         score_matmuls(7, 0)
         half_maximum(6, 1)
         bias_from_maximum(6)
-        inverse_sum(4)
         quantise_e(4)
+        inverse_sum(4)
         half_maximum(7, 0)
         exponentials(5)
         weighted_sum(3, 0)
@@ -400,36 +406,36 @@ def tile_custommodel_pa_kernel(tc, frame_embeddings, tau_global_prime, out):
         divide_and_store(3, 1, False)
         sum_halves(5)
         turn_e(5)
-        group_e(5)
+        group_e(5, nc.vector.tensor_copy)
         score_matmuls(7, 1)
         half_maximum(7, 1)
         bias_from_maximum(7)
-        inverse_sum(5)
         quantise_e(5)
+        inverse_sum(5)
         exponentials(6)
         weighted_sum(4, 0)
         weighted_sum(4, 1)
         divide_and_store(4, 0, False)
-        divide_and_store(4, 1, False)
+        divide_and_store(4, 1, True)
         sum_halves(6)
         turn_e(6)
-        group_e(6)
-        inverse_sum(6)
+        group_e(6, nc.vector.tensor_copy)
         quantise_e(6)
+        inverse_sum(6)
         exponentials(7)
         weighted_sum(5, 0)
         weighted_sum(5, 1)
         divide_and_store(5, 0, False)
-        divide_and_store(5, 1, False)
+        divide_and_store(5, 1, True)
         sum_halves(7)
         turn_e(7)
-        group_e(7)
-        inverse_sum(7)
+        group_e(7, nc.vector.tensor_copy)
         quantise_e(7)
+        inverse_sum(7)
         weighted_sum(6, 0)
         weighted_sum(6, 1)
         divide_and_store(6, 0, False)
-        divide_and_store(6, 1, False)
+        divide_and_store(6, 1, True)
         weighted_sum(7, 0)
         weighted_sum(7, 1)
         divide_and_store(7, 0, False)

@@ -28,7 +28,7 @@ DUOS = SLABS // DUO
 VECTOR_SQUARES = (1,)
 NF_BANKS = (4, 5, 6, 7)
 TURN_BANKS = (7,)
-OUT_BANKS = (3, 6)
+OUT_BANKS = (0, 6)
 FLOPS = 2 * 2 * FRAMES * FRAMES * FEATS
 
 
@@ -90,8 +90,10 @@ def tile_custommodel_pa_kernel(tc, frame_embeddings, tau_global_prime, out):
 
         def score_bank(b, h):
             if h == 0:
-                return b % 3
-            return 6 if b == 2 else 4 + (b + b // 3) % 2
+                return b if b == 0 else 1 + (b - 1) % 3
+            if b == 2:
+                return OUT_BANKS[1]
+            return 4 + (b + (b > 2)) % 2
 
         def score_matmuls(b, h):
             scores[b, h] = bank(score_bank(b, h), [P, BANK])
@@ -323,6 +325,7 @@ def tile_custommodel_pa_kernel(tc, frame_embeddings, tau_global_prime, out):
         score_matmuls(0, 1)
         score_matmuls(1, 1)
         score_matmuls(2, 1)
+        score_matmuls(3, 0)
         temperature()
         half_maximum(0, 1)
         bias_from_maximum(0)
@@ -333,8 +336,8 @@ def tile_custommodel_pa_kernel(tc, frame_embeddings, tau_global_prime, out):
         sum_halves(0)
         exponentials(1)
         turn_e(0)
-        score_matmuls(3, 0)
         score_matmuls(3, 1)
+        score_matmuls(4, 0)
         quantise_f(2)
         group_e(0, nc.scalar.copy)
         half_maximum(2, 0)
@@ -350,7 +353,6 @@ def tile_custommodel_pa_kernel(tc, frame_embeddings, tau_global_prime, out):
         quantise_e(1)
         inverse_sum(0)
         half_maximum(3, 0)
-        score_matmuls(4, 0)
         half_maximum(3, 1)
         bias_from_maximum(3)
         inverse_sum(1)

@@ -127,6 +127,17 @@ def tile_custommodel_pa_kernel(tc, frame_embeddings, tau_global_prime, out):
         nf_grouped = {}
         f_grouped = {}
 
+        def keep_busy(count):
+            unused = bank(3, [P, BANK])
+            for repeat in range(count):
+                nc.tensor.matmul(
+                    out=unused[:],
+                    lhsT=f_sb[:, 0, 0:P],
+                    rhs=f_sb[:, 0, 0:BANK],
+                    start=(repeat == 0),
+                    stop=(repeat == count - 1),
+                )
+
         def sum_of_squares(b):
             total = sumsq[b // DUO][:, b % DUO : b % DUO + 1]
             if b in VECTOR_SQUARES:
@@ -231,14 +242,15 @@ def tile_custommodel_pa_kernel(tc, frame_embeddings, tau_global_prime, out):
         quantise_f(1)
         sum_of_squares(6)
         sum_of_squares(7)
-        regroup_f(2, nc.vector.tensor_copy, 0, BANK)
         roots(3)
         inverse_norms(3)
         group_nf(2, nc.scalar.copy)
+        keep_busy(4)
         normalise_and_turn(6)
         group_nf(3, nc.scalar.copy)
         normalise_and_turn(7)
         quantise_nf(1)
+        regroup_f(2, nc.vector.tensor_copy, 0, BANK)
         group_nf(4, nc.scalar.copy)
         group_nf(5, nc.scalar.copy)
         score_matmuls(0, 0)
@@ -333,8 +345,8 @@ def tile_custommodel_pa_kernel(tc, frame_embeddings, tau_global_prime, out):
         half_maximum(1, 1)
         bias_from_maximum(1)
         exponentials(0)
-        sum_halves(0)
         exponentials(1)
+        sum_halves(0)
         turn_e(0)
         score_matmuls(3, 1)
         score_matmuls(4, 0)

@@ -27,8 +27,9 @@ DUO = 2
 DUOS = SLABS // DUO
 VECTOR_SQUARES = (1,)
 NF_BANKS = (4, 5, 6, 7)
-TURN_BANKS = (7,)
-OUT_BANKS = (0, 6)
+SCORE_RING = (0, 1, 2, 3, 7)
+TURN_BANKS = (4,)
+OUT_BANKS = (5, 6)
 FLOPS = 2 * 2 * FRAMES * FRAMES * FEATS
 
 
@@ -89,11 +90,9 @@ def tile_custommodel_pa_kernel(tc, frame_embeddings, tau_global_prime, out):
         scores = {}
 
         def score_bank(b, h):
-            if h == 0:
-                return b if b == 0 else 1 + (b - 1) % 3
-            if b == 2:
-                return OUT_BANKS[1]
-            return 4 + (b + (b > 2)) % 2
+            if b < PACK:
+                return b + PACK * h
+            return SCORE_RING[(HALVES * (b - PACK) + h) % len(SCORE_RING)]
 
         def score_matmuls(b, h):
             scores[b, h] = bank(score_bank(b, h), [P, BANK])
@@ -333,11 +332,12 @@ def tile_custommodel_pa_kernel(tc, frame_embeddings, tau_global_prime, out):
         quantise_nf(3)
         half_maximum(0, 0)
         temperature_table()
-        regroup_f(3, nc.scalar.copy, 0, BANK // 2)
+        regroup_f(3, nc.scalar.copy, 0, 256)
         score_matmuls(0, 1)
         score_matmuls(1, 1)
         score_matmuls(2, 1)
         score_matmuls(3, 0)
+        score_matmuls(3, 1)
         temperature()
         half_maximum(0, 1)
         bias_from_maximum(0)
@@ -348,41 +348,40 @@ def tile_custommodel_pa_kernel(tc, frame_embeddings, tau_global_prime, out):
         exponentials(1)
         sum_halves(0)
         turn_e(0)
-        score_matmuls(3, 1)
-        score_matmuls(4, 0)
         quantise_f(2)
         group_e(0, nc.scalar.copy)
         half_maximum(2, 0)
         half_maximum(2, 1)
         bias_from_maximum(2)
-        regroup_f(3, nc.vector.tensor_copy, BANK // 2, BANK)
+        score_matmuls(4, 0)
+        regroup_f(3, nc.vector.tensor_copy, 256, BANK)
         quantise_e(0)
         quantise_f(3)
+        inverse_sum(0)
         sum_halves(1)
         exponentials(2)
         turn_e(1)
         group_e(1, nc.scalar.copy)
-        quantise_e(1)
-        inverse_sum(0)
         half_maximum(3, 0)
         half_maximum(3, 1)
         bias_from_maximum(3)
-        inverse_sum(1)
+        quantise_e(1)
         half_maximum(4, 0)
+        score_matmuls(4, 1)
+        half_maximum(4, 1)
+        inverse_sum(1)
+        bias_from_maximum(4)
         weighted_sum(0, 0)
         weighted_sum(0, 1)
         divide_and_store(0, 0, False)
         divide_and_store(0, 1, False)
         sum_halves(2)
         turn_e(2)
-        group_e(2, nc.vector.tensor_copy)
-        score_matmuls(4, 1)
+        group_e(2, nc.scalar.copy)
         score_matmuls(5, 0)
-        half_maximum(4, 1)
-        bias_from_maximum(4)
+        half_maximum(5, 0)
         quantise_e(2)
         inverse_sum(2)
-        half_maximum(5, 0)
         exponentials(3)
         weighted_sum(1, 0)
         weighted_sum(1, 1)
@@ -394,9 +393,9 @@ def tile_custommodel_pa_kernel(tc, frame_embeddings, tau_global_prime, out):
         score_matmuls(5, 1)
         score_matmuls(6, 0)
         half_maximum(5, 1)
-        bias_from_maximum(5)
         quantise_e(3)
         inverse_sum(3)
+        bias_from_maximum(5)
         half_maximum(6, 0)
         exponentials(4)
         weighted_sum(2, 0)
@@ -409,9 +408,9 @@ def tile_custommodel_pa_kernel(tc, frame_embeddings, tau_global_prime, out):
         score_matmuls(6, 1)
         score_matmuls(7, 0)
         half_maximum(6, 1)
-        bias_from_maximum(6)
         quantise_e(4)
         inverse_sum(4)
+        bias_from_maximum(6)
         half_maximum(7, 0)
         exponentials(5)
         weighted_sum(3, 0)
@@ -423,9 +422,9 @@ def tile_custommodel_pa_kernel(tc, frame_embeddings, tau_global_prime, out):
         group_e(5, nc.vector.tensor_copy)
         score_matmuls(7, 1)
         half_maximum(7, 1)
-        bias_from_maximum(7)
         quantise_e(5)
         inverse_sum(5)
+        bias_from_maximum(7)
         exponentials(6)
         weighted_sum(4, 0)
         weighted_sum(4, 1)

@@ -306,12 +306,11 @@ def tile_custommodel_pa_kernel(tc, frame_embeddings, tau_global_prime, out):
 
         acc = {}
 
-        def weighted_sum(b, h):
-            cols = slice(h * BANK, (h + 1) * BANK)
-            acc[b, h] = bank(OUT_BANKS[h], [P, BANK])
+        def weighted_sum(b, cols, number):
+            acc[b, cols.start] = bank(number, [P, cols.stop - cols.start])
             for g in range(PASSES):
                 nc.tensor.matmul_mx(
-                    out=acc[b, h][:],
+                    out=acc[b, cols.start][:],
                     lhsT=e_codes[b][:, g, :].bitcast(FP8X4),
                     lhsT_scale=e_scales[b][:, g, :],
                     rhs=f_codes[:, g, cols].bitcast(FP8X4),
@@ -320,13 +319,12 @@ def tile_custommodel_pa_kernel(tc, frame_embeddings, tau_global_prime, out):
                     stop=(g == PASSES - 1),
                 )
 
-        def divide_and_store(b, h, on_vector):
-            cols = slice(h * BANK, (h + 1) * BANK)
-            result = results.tile([P, BANK], F32, name="result")
+        def divide_and_store(b, cols, on_vector):
+            result = results.tile([P, cols.stop - cols.start], F32, name="result")
             if on_vector:
-                nc.vector.tensor_scalar_mul(out=result[:], in0=acc[b, h][:], scalar1=inv_sum[:, b : b + 1])
+                nc.vector.tensor_scalar_mul(out=result[:], in0=acc[b, cols.start][:], scalar1=inv_sum[:, b : b + 1])
             else:
-                nc.scalar.activation(out=result[:], in_=acc[b, h][:], func=ACT.Copy, scale=inv_sum[:, b : b + 1])
+                nc.scalar.activation(out=result[:], in_=acc[b, cols.start][:], func=ACT.Copy, scale=inv_sum[:, b : b + 1])
             nc.sync.dma_start(out=out_rows[:, b // PACK, b % PACK, cols], in_=result[:])
 
         quantise_nf(3)
@@ -371,10 +369,10 @@ def tile_custommodel_pa_kernel(tc, frame_embeddings, tau_global_prime, out):
         half_maximum(4, 1)
         inverse_sum(1)
         bias_from_maximum(4)
-        weighted_sum(0, 0)
-        weighted_sum(0, 1)
-        divide_and_store(0, 0, False)
-        divide_and_store(0, 1, False)
+        weighted_sum(0, slice(0, BANK), OUT_BANKS[0])
+        weighted_sum(0, slice(BANK, FEATS), OUT_BANKS[1])
+        divide_and_store(0, slice(0, BANK), False)
+        divide_and_store(0, slice(BANK, FEATS), False)
         sum_halves(2)
         turn_e(2)
         group_e(2, nc.scalar.copy)
@@ -383,10 +381,10 @@ def tile_custommodel_pa_kernel(tc, frame_embeddings, tau_global_prime, out):
         quantise_e(2)
         inverse_sum(2)
         exponentials(3)
-        weighted_sum(1, 0)
-        weighted_sum(1, 1)
-        divide_and_store(1, 0, False)
-        divide_and_store(1, 1, False)
+        weighted_sum(1, slice(0, BANK), OUT_BANKS[0])
+        weighted_sum(1, slice(BANK, FEATS), OUT_BANKS[1])
+        divide_and_store(1, slice(0, BANK), False)
+        divide_and_store(1, slice(BANK, FEATS), False)
         sum_halves(3)
         turn_e(3)
         group_e(3, nc.vector.tensor_copy)
@@ -398,10 +396,10 @@ def tile_custommodel_pa_kernel(tc, frame_embeddings, tau_global_prime, out):
         bias_from_maximum(5)
         half_maximum(6, 0)
         exponentials(4)
-        weighted_sum(2, 0)
-        weighted_sum(2, 1)
-        divide_and_store(2, 0, False)
-        divide_and_store(2, 1, False)
+        weighted_sum(2, slice(0, BANK), OUT_BANKS[0])
+        weighted_sum(2, slice(BANK, FEATS), OUT_BANKS[1])
+        divide_and_store(2, slice(0, BANK), False)
+        divide_and_store(2, slice(BANK, FEATS), False)
         sum_halves(4)
         turn_e(4)
         group_e(4, nc.vector.tensor_copy)
@@ -413,10 +411,10 @@ def tile_custommodel_pa_kernel(tc, frame_embeddings, tau_global_prime, out):
         bias_from_maximum(6)
         half_maximum(7, 0)
         exponentials(5)
-        weighted_sum(3, 0)
-        weighted_sum(3, 1)
-        divide_and_store(3, 0, False)
-        divide_and_store(3, 1, False)
+        weighted_sum(3, slice(0, BANK), OUT_BANKS[0])
+        weighted_sum(3, slice(BANK, FEATS), OUT_BANKS[1])
+        divide_and_store(3, slice(0, BANK), False)
+        divide_and_store(3, slice(BANK, FEATS), False)
         sum_halves(5)
         turn_e(5)
         group_e(5, nc.vector.tensor_copy)
@@ -426,30 +424,34 @@ def tile_custommodel_pa_kernel(tc, frame_embeddings, tau_global_prime, out):
         inverse_sum(5)
         bias_from_maximum(7)
         exponentials(6)
-        weighted_sum(4, 0)
-        weighted_sum(4, 1)
-        divide_and_store(4, 0, False)
-        divide_and_store(4, 1, True)
+        weighted_sum(4, slice(0, BANK), OUT_BANKS[0])
+        weighted_sum(4, slice(BANK, FEATS), OUT_BANKS[1])
+        divide_and_store(4, slice(0, BANK), False)
+        divide_and_store(4, slice(BANK, FEATS), True)
         sum_halves(6)
         turn_e(6)
         group_e(6, nc.vector.tensor_copy)
         quantise_e(6)
         inverse_sum(6)
         exponentials(7)
-        weighted_sum(5, 0)
-        weighted_sum(5, 1)
-        divide_and_store(5, 0, False)
-        divide_and_store(5, 1, True)
+        weighted_sum(5, slice(0, BANK), OUT_BANKS[0])
+        weighted_sum(5, slice(BANK, FEATS), OUT_BANKS[1])
+        divide_and_store(5, slice(0, BANK), False)
+        divide_and_store(5, slice(BANK, FEATS), True)
         sum_halves(7)
         turn_e(7)
         group_e(7, nc.vector.tensor_copy)
         quantise_e(7)
         inverse_sum(7)
-        weighted_sum(6, 0)
-        weighted_sum(6, 1)
-        divide_and_store(6, 0, False)
-        divide_and_store(6, 1, True)
-        weighted_sum(7, 0)
-        weighted_sum(7, 1)
-        divide_and_store(7, 0, False)
-        divide_and_store(7, 1, True)
+        weighted_sum(6, slice(0, BANK), OUT_BANKS[0])
+        weighted_sum(6, slice(BANK, FEATS), OUT_BANKS[1])
+        divide_and_store(6, slice(0, BANK), False)
+        divide_and_store(6, slice(BANK, FEATS), True)
+        weighted_sum(7, slice(0, 256), OUT_BANKS[0])
+        weighted_sum(7, slice(256, 512), OUT_BANKS[1])
+        weighted_sum(7, slice(512, 768), SCORE_RING[0])
+        weighted_sum(7, slice(768, 1024), SCORE_RING[1])
+        divide_and_store(7, slice(0, 256), False)
+        divide_and_store(7, slice(256, 512), True)
+        divide_and_store(7, slice(512, 768), False)
+        divide_and_store(7, slice(768, 1024), True)

@@ -158,9 +158,12 @@ def tile_custommodel_pa_kernel(tc, frame_embeddings, tau_global_prime, out):
             cols = slice(duo * DUO, (duo + 1) * DUO)
             nc.scalar.sqrt(out=norm[:, cols], in_=sumsq[duo][:])
 
-        def inverse_norms(duo):
+        def add_eps(duo):
             cols = slice(duo * DUO, (duo + 1) * DUO)
             nc.vector.tensor_scalar_add(out=norm_eps[:, cols], in0=norm[:, cols], scalar1=EPS)
+
+        def invert_norms(duo):
+            cols = slice(duo * DUO, (duo + 1) * DUO)
             nc.vector.reciprocal(out=inv_norm[:, cols], in_=norm_eps[:, cols])
 
         def normalise_and_turn(b):
@@ -178,14 +181,13 @@ def tile_custommodel_pa_kernel(tc, frame_embeddings, tau_global_prime, out):
                 in_=nf_turned[b][:].rearrange("k (g u) r -> k g r u", u=PAIR),
             )
 
-        def quantise_nf(duo):
+        def quantise_nf(duo, g):
             cols = slice(duo * DUO * P, (duo + 1) * DUO * P)
-            for g in range(PASSES):
-                nc.vector.quantize_mx(
-                    out=nf_codes[:, g, cols].bitcast(FP8X4),
-                    scales=nf_scales[:, g, cols],
-                    in_=nf_grouped[duo][:, g, :],
-                )
+            nc.vector.quantize_mx(
+                out=nf_codes[:, g, cols].bitcast(FP8X4),
+                scales=nf_scales[:, g, cols],
+                in_=nf_grouped[duo][:, g, :],
+            )
 
         def regroup_f(piece, copy, first, last):
             g, h = divmod(piece, HALVES)
@@ -211,20 +213,22 @@ def tile_custommodel_pa_kernel(tc, frame_embeddings, tau_global_prime, out):
             nc.scalar.activation(out=inv_tau[:], in_=tau_sb[:], func=ACT.Exp, scale=-1.0)
 
         def temperature():
-            nc.vector.tensor_scalar_mul(out=score_scale[:], in0=inv_tau[:], scalar1=1.0 / 32.0)
             nc.vector.tensor_scalar_mul(out=minus_scale[:], in0=inv_tau[:], scalar1=-1.0 / 32.0)
+            nc.vector.tensor_scalar_mul(out=score_scale[:], in0=inv_tau[:], scalar1=1.0 / 32.0)
 
         sum_of_squares(0)
         sum_of_squares(1)
         sum_of_squares(2)
         roots(0)
         regroup_f(0, nc.vector.tensor_copy, 0, BANK)
-        inverse_norms(0)
+        add_eps(0)
+        invert_norms(0)
         normalise_and_turn(0)
         normalise_and_turn(1)
         sum_of_squares(3)
         roots(1)
-        inverse_norms(1)
+        add_eps(1)
+        invert_norms(1)
         normalise_and_turn(2)
         normalise_and_turn(3)
         sum_of_squares(4)
@@ -234,28 +238,33 @@ def tile_custommodel_pa_kernel(tc, frame_embeddings, tau_global_prime, out):
         group_nf(0, nc.scalar.copy)
         group_nf(1, nc.scalar.copy)
         regroup_f(1, nc.vector.tensor_copy, 0, BANK)
-        inverse_norms(2)
+        add_eps(2)
+        invert_norms(2)
         normalise_and_turn(4)
         normalise_and_turn(5)
-        quantise_nf(0)
+        quantise_nf(0, 0)
+        quantise_nf(0, 1)
         quantise_f(1)
+        group_nf(2, nc.vector.tensor_copy)
         sum_of_squares(6)
         sum_of_squares(7)
         roots(3)
-        inverse_norms(3)
-        group_nf(2, nc.scalar.copy)
+        add_eps(3)
+        invert_norms(3)
         keep_busy(4)
         normalise_and_turn(6)
         group_nf(3, nc.scalar.copy)
         normalise_and_turn(7)
-        quantise_nf(1)
+        quantise_nf(1, 0)
+        quantise_nf(1, 1)
         regroup_f(2, nc.vector.tensor_copy, 0, BANK)
         group_nf(4, nc.scalar.copy)
         group_nf(5, nc.scalar.copy)
         score_matmuls(0, 0)
         score_matmuls(1, 0)
         score_matmuls(2, 0)
-        quantise_nf(2)
+        quantise_nf(2, 0)
+        quantise_nf(2, 1)
         group_nf(6, nc.scalar.copy)
         group_nf(7, nc.scalar.copy)
 
@@ -277,13 +286,13 @@ def tile_custommodel_pa_kernel(tc, frame_embeddings, tau_global_prime, out):
                     accum_out=half_sum[:, b, g : g + 1],
                 )
 
-        def sum_halves(b):
-            nc.scalar.activation(
-                out=row_sum[:, b : b + 1], in_=half_sum[:, b, 0:1], func=ACT.Identity, bias=half_sum[:, b, 1:2]
-            )
+        def sum_halves(duo):
+            slabs = slice(duo * DUO, (duo + 1) * DUO)
+            nc.vector.tensor_add(out=row_sum[:, slabs], in0=half_sum[:, slabs, 0], in1=half_sum[:, slabs, 1])
 
-        def inverse_sum(b):
-            nc.vector.reciprocal(out=inv_sum[:, b : b + 1], in_=row_sum[:, b : b + 1])
+        def inverse_sum(duo):
+            slabs = slice(duo * DUO, (duo + 1) * DUO)
+            nc.vector.reciprocal(out=inv_sum[:, slabs], in_=row_sum[:, slabs])
 
         def turn_e(b):
             e_turned[b] = turn(TURN_BANKS[b % len(TURN_BANKS)], e_rows[b])
@@ -327,7 +336,8 @@ def tile_custommodel_pa_kernel(tc, frame_embeddings, tau_global_prime, out):
                 nc.scalar.activation(out=result[:], in_=acc[b, cols.start][:], func=ACT.Copy, scale=inv_sum[:, b : b + 1])
             nc.sync.dma_start(out=out_rows[:, b // PACK, b % PACK, cols], in_=result[:])
 
-        quantise_nf(3)
+        quantise_nf(3, 0)
+        quantise_nf(3, 1)
         half_maximum(0, 0)
         temperature_table()
         regroup_f(3, nc.scalar.copy, 0, 256)
@@ -336,63 +346,59 @@ def tile_custommodel_pa_kernel(tc, frame_embeddings, tau_global_prime, out):
         score_matmuls(2, 1)
         score_matmuls(3, 0)
         score_matmuls(3, 1)
-        temperature()
         half_maximum(0, 1)
+        temperature()
         bias_from_maximum(0)
         half_maximum(1, 0)
         half_maximum(1, 1)
         bias_from_maximum(1)
         exponentials(0)
         exponentials(1)
-        sum_halves(0)
         turn_e(0)
         quantise_f(2)
         group_e(0, nc.scalar.copy)
         half_maximum(2, 0)
         half_maximum(2, 1)
+        sum_halves(0)
         bias_from_maximum(2)
         score_matmuls(4, 0)
         regroup_f(3, nc.vector.tensor_copy, 256, BANK)
         quantise_e(0)
         quantise_f(3)
         inverse_sum(0)
-        sum_halves(1)
         exponentials(2)
         turn_e(1)
         group_e(1, nc.scalar.copy)
         half_maximum(3, 0)
         half_maximum(3, 1)
-        bias_from_maximum(3)
         quantise_e(1)
+        bias_from_maximum(3)
         half_maximum(4, 0)
         score_matmuls(4, 1)
         half_maximum(4, 1)
-        inverse_sum(1)
-        bias_from_maximum(4)
         weighted_sum(0, slice(0, BANK), OUT_BANKS[0])
         weighted_sum(0, slice(BANK, FEATS), OUT_BANKS[1])
         divide_and_store(0, slice(0, BANK), False)
         divide_and_store(0, slice(BANK, FEATS), False)
-        sum_halves(2)
         turn_e(2)
         group_e(2, nc.scalar.copy)
         score_matmuls(5, 0)
         half_maximum(5, 0)
         quantise_e(2)
-        inverse_sum(2)
+        bias_from_maximum(4)
         exponentials(3)
         weighted_sum(1, slice(0, BANK), OUT_BANKS[0])
         weighted_sum(1, slice(BANK, FEATS), OUT_BANKS[1])
         divide_and_store(1, slice(0, BANK), False)
         divide_and_store(1, slice(BANK, FEATS), False)
-        sum_halves(3)
         turn_e(3)
+        sum_halves(1)
         group_e(3, nc.vector.tensor_copy)
         score_matmuls(5, 1)
         score_matmuls(6, 0)
+        inverse_sum(1)
         half_maximum(5, 1)
         quantise_e(3)
-        inverse_sum(3)
         bias_from_maximum(5)
         half_maximum(6, 0)
         exponentials(4)
@@ -400,14 +406,12 @@ def tile_custommodel_pa_kernel(tc, frame_embeddings, tau_global_prime, out):
         weighted_sum(2, slice(BANK, FEATS), OUT_BANKS[1])
         divide_and_store(2, slice(0, BANK), False)
         divide_and_store(2, slice(BANK, FEATS), False)
-        sum_halves(4)
         turn_e(4)
         group_e(4, nc.vector.tensor_copy)
         score_matmuls(6, 1)
         score_matmuls(7, 0)
         half_maximum(6, 1)
         quantise_e(4)
-        inverse_sum(4)
         bias_from_maximum(6)
         half_maximum(7, 0)
         exponentials(5)
@@ -415,34 +419,32 @@ def tile_custommodel_pa_kernel(tc, frame_embeddings, tau_global_prime, out):
         weighted_sum(3, slice(BANK, FEATS), OUT_BANKS[1])
         divide_and_store(3, slice(0, BANK), False)
         divide_and_store(3, slice(BANK, FEATS), False)
-        sum_halves(5)
         turn_e(5)
+        sum_halves(2)
         group_e(5, nc.vector.tensor_copy)
         score_matmuls(7, 1)
+        inverse_sum(2)
         half_maximum(7, 1)
         quantise_e(5)
-        inverse_sum(5)
         bias_from_maximum(7)
         exponentials(6)
         weighted_sum(4, slice(0, BANK), OUT_BANKS[0])
         weighted_sum(4, slice(BANK, FEATS), OUT_BANKS[1])
         divide_and_store(4, slice(0, BANK), False)
         divide_and_store(4, slice(BANK, FEATS), True)
-        sum_halves(6)
         turn_e(6)
         group_e(6, nc.vector.tensor_copy)
         quantise_e(6)
-        inverse_sum(6)
         exponentials(7)
         weighted_sum(5, slice(0, BANK), OUT_BANKS[0])
         weighted_sum(5, slice(BANK, FEATS), OUT_BANKS[1])
         divide_and_store(5, slice(0, BANK), False)
         divide_and_store(5, slice(BANK, FEATS), True)
-        sum_halves(7)
         turn_e(7)
+        sum_halves(3)
         group_e(7, nc.vector.tensor_copy)
+        inverse_sum(3)
         quantise_e(7)
-        inverse_sum(7)
         weighted_sum(6, slice(0, BANK), OUT_BANKS[0])
         weighted_sum(6, slice(BANK, FEATS), OUT_BANKS[1])
         divide_and_store(6, slice(0, BANK), False)

@@ -436,14 +436,14 @@ def tile_custommodel_pa_kernel(tc, frame_embeddings, tau_global_prime, out):
         group_e(6, nc.vector.tensor_copy)
         quantise_e(6)
         exponentials(7)
+        sum_halves(3)
         weighted_sum(5, slice(0, BANK), OUT_BANKS[0])
         weighted_sum(5, slice(BANK, FEATS), OUT_BANKS[1])
         divide_and_store(5, slice(0, BANK), False)
         divide_and_store(5, slice(BANK, FEATS), True)
-        turn_e(7)
-        sum_halves(3)
-        group_e(7, nc.vector.tensor_copy)
         inverse_sum(3)
+        turn_e(7)
+        group_e(7, nc.vector.tensor_copy)
         quantise_e(7)
         weighted_sum(6, slice(0, BANK), OUT_BANKS[0])
         weighted_sum(6, slice(BANK, FEATS), OUT_BANKS[1])

@@ -40,8 +40,8 @@ def tile_custommodel_pa_kernel(tc, frame_embeddings, tau_global_prime, out):
 
     with ExitStack() as stack:
         keep = stack.enter_context(tc.tile_pool(name="keep", bufs=1))
-        work = stack.enter_context(tc.tile_pool(name="work", bufs=3))
-        results = stack.enter_context(tc.tile_pool(name="results", bufs=8))
+        work = stack.enter_context(tc.tile_pool(name="work", bufs=SLABS))
+        results = stack.enter_context(tc.tile_pool(name="results", bufs=SLABS * HALVES + 2))
         psum = stack.enter_context(tc.psum_pool(name="psum", bufs=1, reuse_waits="tile"))
 
         def bank(number, shape):
@@ -174,7 +174,7 @@ def tile_custommodel_pa_kernel(tc, frame_embeddings, tau_global_prime, out):
         def group_nf(b, copy):
             duo, member = divmod(b, DUO)
             if member == 0:
-                nf_grouped[duo] = work.tile([P, PASSES, DUO * P * PACK], BF16, name="nf_grouped", align_bytes=64)
+                nf_grouped[duo] = work.tile([P, PASSES, DUO * P * PACK], BF16, name="nf_grouped", align_bytes=64, bufs=DUOS)
             cols = slice(member * P * PACK, (member + 1) * P * PACK)
             copy(
                 out=nf_grouped[duo][:, :, cols].bitcast(F32).rearrange("k g (r u) -> k g r u", u=PAIR),
@@ -192,7 +192,7 @@ def tile_custommodel_pa_kernel(tc, frame_embeddings, tau_global_prime, out):
         def regroup_f(piece, copy, first, last):
             g, h = divmod(piece, HALVES)
             if first == 0:
-                f_grouped[piece] = work.tile([P, BANK, PACK], BF16, name="f_grouped", align_bytes=64)
+                f_grouped[piece] = work.tile([P, BANK, PACK], BF16, name="f_grouped", align_bytes=64, bufs=PASSES * HALVES)
             copy(
                 out=f_grouped[piece][:, first:last, :].rearrange("p (c i) t -> p c t i", i=4),
                 in_=f_sb[:, g * PACK : (g + 1) * PACK, h * BANK + first : h * BANK + last].rearrange(
@@ -220,29 +220,31 @@ def tile_custommodel_pa_kernel(tc, frame_embeddings, tau_global_prime, out):
         sum_of_squares(1)
         sum_of_squares(2)
         roots(0)
-        regroup_f(0, nc.vector.tensor_copy, 0, BANK)
+        regroup_f(0, nc.vector.tensor_copy, 0, BANK // 2)
         add_eps(0)
+        regroup_f(0, nc.vector.tensor_copy, BANK // 2, BANK)
         invert_norms(0)
         normalise_and_turn(0)
         normalise_and_turn(1)
         sum_of_squares(3)
         roots(1)
         add_eps(1)
+        quantise_f(0)
         invert_norms(1)
+        regroup_f(1, nc.vector.tensor_copy, 0, BANK)
         normalise_and_turn(2)
         normalise_and_turn(3)
         sum_of_squares(4)
         sum_of_squares(5)
         roots(2)
-        quantise_f(0)
         group_nf(0, nc.scalar.copy)
         group_nf(1, nc.scalar.copy)
-        regroup_f(1, nc.vector.tensor_copy, 0, BANK)
         add_eps(2)
+        regroup_f(2, nc.vector.tensor_copy, 0, BANK // 2)
         invert_norms(2)
+        quantise_nf(0, 0)
         normalise_and_turn(4)
         normalise_and_turn(5)
-        quantise_nf(0, 0)
         quantise_nf(0, 1)
         quantise_f(1)
         group_nf(2, nc.vector.tensor_copy)
@@ -251,13 +253,13 @@ def tile_custommodel_pa_kernel(tc, frame_embeddings, tau_global_prime, out):
         roots(3)
         add_eps(3)
         invert_norms(3)
-        keep_busy(4)
+        keep_busy(2)
         normalise_and_turn(6)
         group_nf(3, nc.scalar.copy)
         normalise_and_turn(7)
         quantise_nf(1, 0)
         quantise_nf(1, 1)
-        regroup_f(2, nc.vector.tensor_copy, 0, BANK)
+        regroup_f(2, nc.vector.tensor_copy, BANK // 2, BANK)
         group_nf(4, nc.scalar.copy)
         group_nf(5, nc.scalar.copy)
         score_matmuls(0, 0)

@@ -25,12 +25,17 @@ CHUNKS = FEATS // (PAIR * P)
 EPS = 1e-6
 DUO = 2
 DUOS = SLABS // DUO
-VECTOR_SQUARES = (1,)
-NF_BANKS = (4, 5, 6, 7)
-SCORE_RING = (0, 1, 2, 3, 7)
-TURN_BANKS = (4,)
-OUT_BANKS = (5, 6)
 FLOPS = 2 * 2 * FRAMES * FRAMES * FEATS
+
+NF_BANKS = (4, 5, 6, 7)
+WARM_BANK = 3
+TURN_BANK = 4
+SUM_BANKS = (5, 6)
+SCORE_RING = (0, 1, 2, 3, 7)
+RING_OWNERS = (0, 1, 2, 3, 3)
+
+LATE = SLABS // 2
+SCALAR_COPIES = (0, 1, 2)
 
 
 def tile_custommodel_pa_kernel(tc, frame_embeddings, tau_global_prime, out):
@@ -80,66 +85,16 @@ def tile_custommodel_pa_kernel(tc, frame_embeddings, tau_global_prime, out):
         nc.vector.memset(one[:], 1.0)
         nc.scalar.sqrt(out=root_of_one[:], in_=one[:])
 
-        def turn(number, rows):
-            words = rows[:].bitcast(F32)
-            turned = bank(number, [P, CHUNKS, P])
-            for q in range(CHUNKS):
-                nc.tensor.transpose(turned[:, q, :], words[:, q * P : (q + 1) * P], ident[:])
-            return turned
+        def load_temperature():
+            nc.scalar.activation(out=inv_tau[:], in_=tau_sb[:], func=ACT.Exp, scale=-1.0)
 
-        scores = {}
-
-        def score_bank(b, h):
-            if b < PACK:
-                return b + PACK * h
-            return SCORE_RING[(HALVES * (b - PACK) + h) % len(SCORE_RING)]
-
-        def score_matmuls(b, h):
-            scores[b, h] = bank(score_bank(b, h), [P, BANK])
-            rows = slice(b * P, (b + 1) * P)
-            cols = slice(h * BANK, (h + 1) * BANK)
-            for g in range(PASSES):
-                nc.tensor.matmul_mx(
-                    out=scores[b, h][:],
-                    lhsT=nf_codes[:, g, rows].bitcast(FP8X4),
-                    lhsT_scale=nf_scales[:, g, rows],
-                    rhs=nf_codes[:, g, cols].bitcast(FP8X4),
-                    rhs_scale=nf_scales[:, g, cols],
-                    start=(g == 0),
-                    stop=(g == PASSES - 1),
-                )
-
-        def half_maximum(b, h):
-            nc.vector.reduce_max(out=half_max[:, b, h : h + 1], in_=scores[b, h][:], axis=AXIS.X)
-
-        def bias_from_maximum(b):
-            nc.vector.tensor_scalar(
-                out=exp_bias[:, b : b + 1],
-                in0=half_max[:, b, 0:1],
-                scalar1=half_max[:, b, 1:2],
-                scalar2=minus_scale[:, 0:1],
-                op0=ALU.max,
-                op1=ALU.mult,
-            )
-
-        nf_turned = {}
-        nf_grouped = {}
-        f_grouped = {}
-
-        def keep_busy(count):
-            unused = bank(3, [P, BANK])
-            for repeat in range(count):
-                nc.tensor.matmul(
-                    out=unused[:],
-                    lhsT=f_sb[:, 0, 0:P],
-                    rhs=f_sb[:, 0, 0:BANK],
-                    start=(repeat == 0),
-                    stop=(repeat == count - 1),
-                )
+        def scale_temperature():
+            nc.vector.tensor_scalar_mul(out=minus_scale[:], in0=inv_tau[:], scalar1=-1.0 / 32.0)
+            nc.vector.tensor_scalar_mul(out=score_scale[:], in0=inv_tau[:], scalar1=1.0 / 32.0)
 
         def sum_of_squares(b):
             total = sumsq[b // DUO][:, b % DUO : b % DUO + 1]
-            if b in VECTOR_SQUARES:
+            if b == 1:
                 squares = work.tile([P, FEATS], BF16, name="vector_squares")
                 nc.vector.scalar_tensor_tensor(
                     out=squares[:],
@@ -166,15 +121,27 @@ def tile_custommodel_pa_kernel(tc, frame_embeddings, tau_global_prime, out):
             cols = slice(duo * DUO, (duo + 1) * DUO)
             nc.vector.reciprocal(out=inv_norm[:, cols], in_=norm_eps[:, cols])
 
+        def turn(turned, rows, first_chunk, chunks):
+            words = rows[:].bitcast(F32)
+            for c in range(chunks):
+                q = first_chunk + c
+                nc.tensor.transpose(turned[:, c, :], words[:, q * P : (q + 1) * P], ident[:])
+
+        nf_turned = {}
+        nf_grouped = {}
+
         def normalise_and_turn(b):
             nf = work.tile([P, FEATS], BF16, name="nf")
             nc.vector.tensor_scalar_mul(out=nf[:], in0=f_sb[:, b, :], scalar1=inv_norm[:, b : b + 1])
-            nf_turned[b] = turn(NF_BANKS[b % len(NF_BANKS)], nf)
+            nf_turned[b] = bank(NF_BANKS[b % len(NF_BANKS)], [P, CHUNKS, P])
+            turn(nf_turned[b], nf, 0, CHUNKS)
 
         def group_nf(b, copy):
             duo, member = divmod(b, DUO)
             if member == 0:
-                nf_grouped[duo] = work.tile([P, PASSES, DUO * P * PACK], BF16, name="nf_grouped", align_bytes=64, bufs=DUOS)
+                nf_grouped[duo] = work.tile(
+                    [P, PASSES, DUO * P * PACK], BF16, name="nf_grouped", align_bytes=64, bufs=DUOS
+                )
             cols = slice(member * P * PACK, (member + 1) * P * PACK)
             copy(
                 out=nf_grouped[duo][:, :, cols].bitcast(F32).rearrange("k g (r u) -> k g r u", u=PAIR),
@@ -189,10 +156,25 @@ def tile_custommodel_pa_kernel(tc, frame_embeddings, tau_global_prime, out):
                 in_=nf_grouped[duo][:, g, :],
             )
 
-        def regroup_f(piece, copy, first, last):
+        def warm_up(count):
+            unused = bank(WARM_BANK, [P, BANK])
+            for repeat in range(count):
+                nc.tensor.matmul(
+                    out=unused[:],
+                    lhsT=f_sb[:, 0, 0:P],
+                    rhs=f_sb[:, 0, 0:BANK],
+                    start=(repeat == 0),
+                    stop=(repeat == count - 1),
+                )
+
+        f_grouped = {}
+
+        def regroup_f(piece, copy, first=0, last=BANK):
             g, h = divmod(piece, HALVES)
             if first == 0:
-                f_grouped[piece] = work.tile([P, BANK, PACK], BF16, name="f_grouped", align_bytes=64, bufs=PASSES * HALVES)
+                f_grouped[piece] = work.tile(
+                    [P, BANK, PACK], BF16, name="f_grouped", align_bytes=64, bufs=PASSES * HALVES
+                )
             copy(
                 out=f_grouped[piece][:, first:last, :].rearrange("p (c i) t -> p c t i", i=4),
                 in_=f_sb[:, g * PACK : (g + 1) * PACK, h * BANK + first : h * BANK + last].rearrange(
@@ -209,66 +191,39 @@ def tile_custommodel_pa_kernel(tc, frame_embeddings, tau_global_prime, out):
                 in_=f_grouped[piece][:].rearrange("p d t -> p (d t)"),
             )
 
-        def temperature_table():
-            nc.scalar.activation(out=inv_tau[:], in_=tau_sb[:], func=ACT.Exp, scale=-1.0)
+        scores = {}
 
-        def temperature():
-            nc.vector.tensor_scalar_mul(out=minus_scale[:], in0=inv_tau[:], scalar1=-1.0 / 32.0)
-            nc.vector.tensor_scalar_mul(out=score_scale[:], in0=inv_tau[:], scalar1=1.0 / 32.0)
+        def ring_index(b, h):
+            return HALVES * (b - PACK) + h
 
-        sum_of_squares(0)
-        sum_of_squares(1)
-        sum_of_squares(2)
-        roots(0)
-        regroup_f(0, nc.vector.tensor_copy, 0, BANK // 2)
-        add_eps(0)
-        regroup_f(0, nc.vector.tensor_copy, BANK // 2, BANK)
-        invert_norms(0)
-        normalise_and_turn(0)
-        normalise_and_turn(1)
-        sum_of_squares(3)
-        roots(1)
-        add_eps(1)
-        quantise_f(0)
-        invert_norms(1)
-        regroup_f(1, nc.vector.tensor_copy, 0, BANK)
-        normalise_and_turn(2)
-        normalise_and_turn(3)
-        sum_of_squares(4)
-        sum_of_squares(5)
-        roots(2)
-        group_nf(0, nc.scalar.copy)
-        group_nf(1, nc.scalar.copy)
-        add_eps(2)
-        regroup_f(2, nc.vector.tensor_copy, 0, BANK // 2)
-        invert_norms(2)
-        quantise_nf(0, 0)
-        normalise_and_turn(4)
-        normalise_and_turn(5)
-        quantise_nf(0, 1)
-        quantise_f(1)
-        group_nf(2, nc.vector.tensor_copy)
-        sum_of_squares(6)
-        sum_of_squares(7)
-        roots(3)
-        add_eps(3)
-        invert_norms(3)
-        keep_busy(2)
-        normalise_and_turn(6)
-        group_nf(3, nc.scalar.copy)
-        normalise_and_turn(7)
-        quantise_nf(1, 0)
-        quantise_nf(1, 1)
-        regroup_f(2, nc.vector.tensor_copy, BANK // 2, BANK)
-        group_nf(4, nc.scalar.copy)
-        group_nf(5, nc.scalar.copy)
-        score_matmuls(0, 0)
-        score_matmuls(1, 0)
-        score_matmuls(2, 0)
-        quantise_nf(2, 0)
-        quantise_nf(2, 1)
-        group_nf(6, nc.scalar.copy)
-        group_nf(7, nc.scalar.copy)
+        def score_matmuls(b, h):
+            number = b + PACK * h if b < PACK else SCORE_RING[ring_index(b, h) % len(SCORE_RING)]
+            scores[b, h] = bank(number, [P, BANK])
+            rows = slice(b * P, (b + 1) * P)
+            cols = slice(h * BANK, (h + 1) * BANK)
+            for g in range(PASSES):
+                nc.tensor.matmul_mx(
+                    out=scores[b, h][:],
+                    lhsT=nf_codes[:, g, rows].bitcast(FP8X4),
+                    lhsT_scale=nf_scales[:, g, rows],
+                    rhs=nf_codes[:, g, cols].bitcast(FP8X4),
+                    rhs_scale=nf_scales[:, g, cols],
+                    start=(g == 0),
+                    stop=(g == PASSES - 1),
+                )
+
+        def half_maximum(b, h):
+            nc.vector.reduce_max(out=half_max[:, b, h : h + 1], in_=scores[b, h][:], axis=AXIS.X)
+
+        def bias_from_maximum(b):
+            nc.vector.tensor_scalar(
+                out=exp_bias[:, b : b + 1],
+                in0=half_max[:, b, 0:1],
+                scalar1=half_max[:, b, 1:2],
+                scalar2=minus_scale[:, 0:1],
+                op0=ALU.max,
+                op1=ALU.mult,
+            )
 
         e_rows = {}
         e_turned = {}
@@ -288,16 +243,17 @@ def tile_custommodel_pa_kernel(tc, frame_embeddings, tau_global_prime, out):
                     accum_out=half_sum[:, b, g : g + 1],
                 )
 
-        def sum_halves(duo):
+        def add_half_sums(duo):
             slabs = slice(duo * DUO, (duo + 1) * DUO)
             nc.vector.tensor_add(out=row_sum[:, slabs], in0=half_sum[:, slabs, 0], in1=half_sum[:, slabs, 1])
 
-        def inverse_sum(duo):
+        def invert_sums(duo):
             slabs = slice(duo * DUO, (duo + 1) * DUO)
             nc.vector.reciprocal(out=inv_sum[:, slabs], in_=row_sum[:, slabs])
 
         def turn_e(b):
-            e_turned[b] = turn(TURN_BANKS[b % len(TURN_BANKS)], e_rows[b])
+            e_turned[b] = bank(TURN_BANK, [P, CHUNKS, P])
+            turn(e_turned[b], e_rows[b], 0, CHUNKS)
 
         def group_e(b, copy):
             e_grouped[b] = work.tile([P, PASSES * P * PACK], BF16, name="e_grouped", align_bytes=64)
@@ -306,22 +262,44 @@ def tile_custommodel_pa_kernel(tc, frame_embeddings, tau_global_prime, out):
                 in_=e_turned[b][:].rearrange("k (g u) r -> k g r u", u=PAIR),
             )
 
-        def quantise_e(b):
+        def new_e_operand(b):
             e_codes[b] = work.tile([P, PASSES, P], U32, name="e_codes", align_bytes=64)
             e_scales[b] = work.tile([P, PASSES, P], U8, name="e_scales", align_bytes=64)
+
+        def quantise_e(b):
+            new_e_operand(b)
             nc.vector.quantize_mx(
                 out=e_codes[b][:].rearrange("p g i -> p (g i)").bitcast(FP8X4),
                 scales=e_scales[b][:].rearrange("p g i -> p (g i)"),
                 in_=e_grouped[b][:],
             )
 
-        acc = {}
+        def turn_group_and_quantise_last_e(b):
+            for g, number in enumerate((TURN_BANK, SCORE_RING[-1])):
+                e_turned[b, g] = bank(number, [P, PAIR, P])
+                turn(e_turned[b, g], e_rows[b], g * PAIR, PAIR)
+            e_grouped[b] = work.tile([P, PASSES * P * PACK], BF16, name="e_grouped", align_bytes=64)
+            for g, copy in enumerate((nc.vector.tensor_copy, nc.scalar.copy)):
+                cols = slice(g * P * PACK, (g + 1) * P * PACK)
+                copy(
+                    out=e_grouped[b][:, cols].bitcast(F32).rearrange("k (r u) -> k r u", u=PAIR),
+                    in_=e_turned[b, g][:].rearrange("k u r -> k r u"),
+                )
+            new_e_operand(b)
+            for g in range(PASSES):
+                nc.vector.quantize_mx(
+                    out=e_codes[b][:, g, :].bitcast(FP8X4),
+                    scales=e_scales[b][:, g, :],
+                    in_=e_grouped[b][:, g * P * PACK : (g + 1) * P * PACK],
+                )
+
+        sums = {}
 
         def weighted_sum(b, cols, number):
-            acc[b, cols.start] = bank(number, [P, cols.stop - cols.start])
+            sums[b, cols.start] = bank(number, [P, cols.stop - cols.start])
             for g in range(PASSES):
                 nc.tensor.matmul_mx(
-                    out=acc[b, cols.start][:],
+                    out=sums[b, cols.start][:],
                     lhsT=e_codes[b][:, g, :].bitcast(FP8X4),
                     lhsT_scale=e_scales[b][:, g, :],
                     rhs=f_codes[:, g, cols].bitcast(FP8X4),
@@ -332,130 +310,158 @@ def tile_custommodel_pa_kernel(tc, frame_embeddings, tau_global_prime, out):
 
         def divide_and_store(b, cols, on_vector):
             result = results.tile([P, cols.stop - cols.start], F32, name="result")
+            source = sums[b, cols.start]
             if on_vector:
-                nc.vector.tensor_scalar_mul(out=result[:], in0=acc[b, cols.start][:], scalar1=inv_sum[:, b : b + 1])
+                nc.vector.tensor_scalar_mul(out=result[:], in0=source[:], scalar1=inv_sum[:, b : b + 1])
             else:
-                nc.scalar.activation(out=result[:], in_=acc[b, cols.start][:], func=ACT.Copy, scale=inv_sum[:, b : b + 1])
+                nc.scalar.activation(out=result[:], in_=source[:], func=ACT.Copy, scale=inv_sum[:, b : b + 1])
             nc.sync.dma_start(out=out_rows[:, b // PACK, b % PACK, cols], in_=result[:])
 
+        def weighted_sums_and_divisions(b):
+            for h in range(HALVES):
+                weighted_sum(b, slice(h * BANK, (h + 1) * BANK), SUM_BANKS[h])
+            divide_and_store(b, slice(0, BANK), False)
+            divide_and_store(b, slice(BANK, FEATS), b >= LATE)
+
+        def last_weighted_sums_and_divisions(b):
+            quarters = []
+            for n in range(4):
+                quarters.append(slice(n * FEATS // 4, (n + 1) * FEATS // 4))
+            for n in range(4):
+                weighted_sum(b, quarters[n], SCORE_RING[n])
+            for n in range(4):
+                divide_and_store(b, quarters[n], n % 2 == 1)
+
+        vector_copy = nc.vector.tensor_copy
+        scalar_copy = nc.scalar.copy
+        middle = BANK // 2
+
+        sum_of_squares(0)
+        sum_of_squares(1)
+        sum_of_squares(2)
+        roots(0)
+        regroup_f(0, vector_copy, last=middle)
+        add_eps(0)
+        regroup_f(0, vector_copy, first=middle)
+        invert_norms(0)
+        normalise_and_turn(0)
+        normalise_and_turn(1)
+        sum_of_squares(3)
+        roots(1)
+        add_eps(1)
+        quantise_f(0)
+        invert_norms(1)
+        regroup_f(1, vector_copy)
+        normalise_and_turn(2)
+        normalise_and_turn(3)
+        sum_of_squares(4)
+        sum_of_squares(5)
+        roots(2)
+        group_nf(0, scalar_copy)
+        group_nf(1, scalar_copy)
+        add_eps(2)
+        regroup_f(2, vector_copy, last=middle)
+        invert_norms(2)
+        quantise_nf(0, 0)
+        normalise_and_turn(4)
+        normalise_and_turn(5)
+        quantise_nf(0, 1)
+        quantise_f(1)
+        group_nf(2, vector_copy)
+        sum_of_squares(6)
+        sum_of_squares(7)
+        roots(3)
+        add_eps(3)
+        invert_norms(3)
+        warm_up(3)
+        normalise_and_turn(6)
+        group_nf(3, scalar_copy)
+        normalise_and_turn(7)
+        quantise_nf(1, 0)
+        quantise_nf(1, 1)
+        regroup_f(2, vector_copy, first=middle)
+        group_nf(4, scalar_copy)
+        group_nf(5, scalar_copy)
+        for b in range(3):
+            score_matmuls(b, 0)
+        quantise_nf(2, 0)
+        quantise_nf(2, 1)
+        group_nf(6, scalar_copy)
+        group_nf(7, scalar_copy)
         quantise_nf(3, 0)
         quantise_nf(3, 1)
+
         half_maximum(0, 0)
-        temperature_table()
-        regroup_f(3, nc.scalar.copy, 0, 256)
-        score_matmuls(0, 1)
-        score_matmuls(1, 1)
-        score_matmuls(2, 1)
+        load_temperature()
+        regroup_f(3, scalar_copy, last=middle)
+        for b in range(3):
+            score_matmuls(b, 1)
         score_matmuls(3, 0)
         score_matmuls(3, 1)
         half_maximum(0, 1)
-        temperature()
+        scale_temperature()
         bias_from_maximum(0)
         half_maximum(1, 0)
         half_maximum(1, 1)
         bias_from_maximum(1)
         exponentials(0)
         exponentials(1)
+
         turn_e(0)
         quantise_f(2)
-        group_e(0, nc.scalar.copy)
+        group_e(0, scalar_copy)
         half_maximum(2, 0)
         half_maximum(2, 1)
-        sum_halves(0)
+        add_half_sums(0)
         bias_from_maximum(2)
         score_matmuls(4, 0)
-        regroup_f(3, nc.vector.tensor_copy, 256, BANK)
+        regroup_f(3, vector_copy, first=middle)
         quantise_e(0)
         quantise_f(3)
-        inverse_sum(0)
+        invert_sums(0)
+        score_matmuls(4, 1)
         exponentials(2)
         turn_e(1)
-        group_e(1, nc.scalar.copy)
+        group_e(1, scalar_copy)
         half_maximum(3, 0)
         half_maximum(3, 1)
         quantise_e(1)
         bias_from_maximum(3)
         half_maximum(4, 0)
-        score_matmuls(4, 1)
         half_maximum(4, 1)
-        weighted_sum(0, slice(0, BANK), OUT_BANKS[0])
-        weighted_sum(0, slice(BANK, FEATS), OUT_BANKS[1])
-        divide_and_store(0, slice(0, BANK), False)
-        divide_and_store(0, slice(BANK, FEATS), False)
-        turn_e(2)
-        group_e(2, nc.scalar.copy)
-        score_matmuls(5, 0)
-        half_maximum(5, 0)
-        quantise_e(2)
-        bias_from_maximum(4)
-        exponentials(3)
-        weighted_sum(1, slice(0, BANK), OUT_BANKS[0])
-        weighted_sum(1, slice(BANK, FEATS), OUT_BANKS[1])
-        divide_and_store(1, slice(0, BANK), False)
-        divide_and_store(1, slice(BANK, FEATS), False)
-        turn_e(3)
-        sum_halves(1)
-        group_e(3, nc.vector.tensor_copy)
-        score_matmuls(5, 1)
-        score_matmuls(6, 0)
-        inverse_sum(1)
-        half_maximum(5, 1)
-        quantise_e(3)
-        bias_from_maximum(5)
-        half_maximum(6, 0)
-        exponentials(4)
-        weighted_sum(2, slice(0, BANK), OUT_BANKS[0])
-        weighted_sum(2, slice(BANK, FEATS), OUT_BANKS[1])
-        divide_and_store(2, slice(0, BANK), False)
-        divide_and_store(2, slice(BANK, FEATS), False)
-        turn_e(4)
-        group_e(4, nc.vector.tensor_copy)
-        score_matmuls(6, 1)
-        score_matmuls(7, 0)
-        half_maximum(6, 1)
-        quantise_e(4)
-        bias_from_maximum(6)
-        half_maximum(7, 0)
-        exponentials(5)
-        weighted_sum(3, slice(0, BANK), OUT_BANKS[0])
-        weighted_sum(3, slice(BANK, FEATS), OUT_BANKS[1])
-        divide_and_store(3, slice(0, BANK), False)
-        divide_and_store(3, slice(BANK, FEATS), False)
-        turn_e(5)
-        sum_halves(2)
-        group_e(5, nc.vector.tensor_copy)
-        score_matmuls(7, 1)
-        inverse_sum(2)
-        half_maximum(7, 1)
-        quantise_e(5)
-        bias_from_maximum(7)
-        exponentials(6)
-        weighted_sum(4, slice(0, BANK), OUT_BANKS[0])
-        weighted_sum(4, slice(BANK, FEATS), OUT_BANKS[1])
-        divide_and_store(4, slice(0, BANK), False)
-        divide_and_store(4, slice(BANK, FEATS), True)
-        turn_e(6)
-        group_e(6, nc.vector.tensor_copy)
-        quantise_e(6)
-        exponentials(7)
-        sum_halves(3)
-        weighted_sum(5, slice(0, BANK), OUT_BANKS[0])
-        weighted_sum(5, slice(BANK, FEATS), OUT_BANKS[1])
-        divide_and_store(5, slice(0, BANK), False)
-        divide_and_store(5, slice(BANK, FEATS), True)
-        inverse_sum(3)
-        turn_e(7)
-        group_e(7, nc.vector.tensor_copy)
-        quantise_e(7)
-        weighted_sum(6, slice(0, BANK), OUT_BANKS[0])
-        weighted_sum(6, slice(BANK, FEATS), OUT_BANKS[1])
-        divide_and_store(6, slice(0, BANK), False)
-        divide_and_store(6, slice(BANK, FEATS), True)
-        weighted_sum(7, slice(0, 256), OUT_BANKS[0])
-        weighted_sum(7, slice(256, 512), OUT_BANKS[1])
-        weighted_sum(7, slice(512, 768), SCORE_RING[0])
-        weighted_sum(7, slice(768, 1024), SCORE_RING[1])
-        divide_and_store(7, slice(0, 256), False)
-        divide_and_store(7, slice(256, 512), True)
-        divide_and_store(7, slice(512, 768), False)
-        divide_and_store(7, slice(768, 1024), True)
+        weighted_sums_and_divisions(0)
+
+        new_scores = {}
+        for b in range(PACK, SLABS):
+            for h in range(HALVES):
+                n = ring_index(b, h)
+                ring = len(SCORE_RING)
+                owner = RING_OWNERS[n] if n < ring else PACK + (n - ring) // HALVES
+                new_scores.setdefault(owner, []).append((b, h))
+        last = SLABS - 1
+        for b in range(2, last):
+            sums_ready = b % DUO == 1
+            fresh = new_scores.get(b, [])
+            turn_e(b)
+            if sums_ready:
+                add_half_sums(b // DUO)
+            group_e(b, scalar_copy if b in SCALAR_COPIES else vector_copy)
+            for tile in fresh:
+                score_matmuls(*tile)
+            if sums_ready:
+                invert_sums(b // DUO)
+            for tile in fresh[:1]:
+                half_maximum(*tile)
+            quantise_e(b)
+            if b + 2 < SLABS:
+                bias_from_maximum(b + 2)
+            for tile in fresh[1:]:
+                half_maximum(*tile)
+            exponentials(b + 1)
+            if b + 1 == last:
+                add_half_sums(last // DUO)
+            weighted_sums_and_divisions(b - 1)
+        invert_sums(last // DUO)
+        turn_group_and_quantise_last_e(last)
+        weighted_sums_and_divisions(last - 1)
+        last_weighted_sums_and_divisions(last)

@@ -69,6 +69,7 @@ def tile_custommodel_pa_kernel(tc, frame_embeddings, tau_global_prime, out):
         norm = keep.tile([P, SLABS], F32)
         root_of_one = keep.tile([P, 1], F32)
         one = keep.tile([P, 1], F32)
+        late_one = keep.tile([P, 1], F32)
         norm_eps = keep.tile([P, SLABS], F32)
         inv_norm = keep.tile([P, SLABS], F32)
         inv_sum = keep.tile([P, SLABS], F32)
@@ -181,6 +182,26 @@ def tile_custommodel_pa_kernel(tc, frame_embeddings, tau_global_prime, out):
                     "p t (c i) -> p c t i", i=4
                 ),
             )
+
+        def regroup_f_on_gpsimd(piece, parts):
+            g, h = divmod(piece, HALVES)
+            f_grouped[piece] = work.tile(
+                [P, BANK, PACK], BF16, name="f_grouped", align_bytes=64, bufs=PASSES * HALVES
+            )
+            width = BANK // parts
+            for n in range(parts):
+                first = n * width
+                last = first + width
+                nc.gpsimd.tensor_scalar(
+                    out=f_grouped[piece][:, first:last, :].rearrange("p (c i) t -> p c t i", i=4),
+                    in0=f_sb[:, g * PACK : (g + 1) * PACK, h * BANK + first : h * BANK + last].rearrange(
+                        "p t (c i) -> p c t i", i=4
+                    ),
+                    scalar1=late_one[:, 0:1],
+                    scalar2=1.0,
+                    op0=ALU.mult,
+                    op1=ALU.mult,
+                )
 
         def quantise_f(piece):
             g, h = divmod(piece, HALVES)
@@ -393,7 +414,8 @@ def tile_custommodel_pa_kernel(tc, frame_embeddings, tau_global_prime, out):
 
         half_maximum(0, 0)
         load_temperature()
-        regroup_f(3, scalar_copy, last=middle)
+        nc.scalar.copy(out=late_one[:], in_=one[:])
+        regroup_f_on_gpsimd(3, 4)
         for b in range(3):
             score_matmuls(b, 1)
         score_matmuls(3, 0)
@@ -415,7 +437,6 @@ def tile_custommodel_pa_kernel(tc, frame_embeddings, tau_global_prime, out):
         add_half_sums(0)
         bias_from_maximum(2)
         score_matmuls(4, 0)
-        regroup_f(3, vector_copy, first=middle)
         quantise_e(0)
         quantise_f(3)
         invert_sums(0)

@@ -28,12 +28,12 @@ DUOS = SLABS // DUO
 FLOPS = 2 * 2 * FRAMES * FRAMES * FEATS
 
 NF_BANKS = (4, 5, 6, 7)
-WARM_BANK = 3
 TURN_BANK = 4
 SUM_BANKS = (5, 6)
 SCORE_RING = (0, 1, 2, 3, 7)
 RING_OWNERS = (0, 1, 2, 3, 3)
 
+VECTOR_SQUARES = (1, 3)
 LATE = SLABS // 2
 SCALAR_COPIES = (0, 1, 2)
 
@@ -95,7 +95,7 @@ def tile_custommodel_pa_kernel(tc, frame_embeddings, tau_global_prime, out):
 
         def sum_of_squares(b):
             total = sumsq[b // DUO][:, b % DUO : b % DUO + 1]
-            if b == 1:
+            if b in VECTOR_SQUARES:
                 squares = work.tile([P, FEATS], BF16, name="vector_squares")
                 nc.vector.scalar_tensor_tensor(
                     out=squares[:],
@@ -157,25 +157,12 @@ def tile_custommodel_pa_kernel(tc, frame_embeddings, tau_global_prime, out):
                 in_=nf_grouped[duo][:, g, :],
             )
 
-        def warm_up(count):
-            unused = bank(WARM_BANK, [P, BANK])
-            for repeat in range(count):
-                nc.tensor.matmul(
-                    out=unused[:],
-                    lhsT=f_sb[:, 0, 0:P],
-                    rhs=f_sb[:, 0, 0:BANK],
-                    start=(repeat == 0),
-                    stop=(repeat == count - 1),
-                )
-
         f_grouped = {}
+        for piece in range(PASSES * HALVES):
+            f_grouped[piece] = keep.tile([P, BANK, PACK], BF16, name="f_grouped%d" % piece, align_bytes=64)
 
         def regroup_f(piece, copy, first=0, last=BANK):
             g, h = divmod(piece, HALVES)
-            if first == 0:
-                f_grouped[piece] = work.tile(
-                    [P, BANK, PACK], BF16, name="f_grouped", align_bytes=64, bufs=PASSES * HALVES
-                )
             copy(
                 out=f_grouped[piece][:, first:last, :].rearrange("p (c i) t -> p c t i", i=4),
                 in_=f_sb[:, g * PACK : (g + 1) * PACK, h * BANK + first : h * BANK + last].rearrange(
@@ -183,25 +170,18 @@ def tile_custommodel_pa_kernel(tc, frame_embeddings, tau_global_prime, out):
                 ),
             )
 
-        def regroup_f_on_gpsimd(piece, parts):
+        def regroup_f_on_gpsimd(piece, first=0, last=BANK):
             g, h = divmod(piece, HALVES)
-            f_grouped[piece] = work.tile(
-                [P, BANK, PACK], BF16, name="f_grouped", align_bytes=64, bufs=PASSES * HALVES
+            nc.gpsimd.tensor_scalar(
+                out=f_grouped[piece][:, first:last, :].rearrange("p (c i) t -> p c t i", i=4),
+                in0=f_sb[:, g * PACK : (g + 1) * PACK, h * BANK + first : h * BANK + last].rearrange(
+                    "p t (c i) -> p c t i", i=4
+                ),
+                scalar1=late_one[:, 0:1],
+                scalar2=1.0,
+                op0=ALU.mult,
+                op1=ALU.mult,
             )
-            width = BANK // parts
-            for n in range(parts):
-                first = n * width
-                last = first + width
-                nc.gpsimd.tensor_scalar(
-                    out=f_grouped[piece][:, first:last, :].rearrange("p (c i) t -> p c t i", i=4),
-                    in0=f_sb[:, g * PACK : (g + 1) * PACK, h * BANK + first : h * BANK + last].rearrange(
-                        "p t (c i) -> p c t i", i=4
-                    ),
-                    scalar1=late_one[:, 0:1],
-                    scalar2=1.0,
-                    op0=ALU.mult,
-                    op1=ALU.mult,
-                )
 
         def quantise_f(piece):
             g, h = divmod(piece, HALVES)
@@ -217,14 +197,16 @@ def tile_custommodel_pa_kernel(tc, frame_embeddings, tau_global_prime, out):
         def ring_index(b, h):
             return HALVES * (b - PACK) + h
 
-        def score_matmuls(b, h):
+        def open_scores(b, h):
             number = b + PACK * h if b < PACK else SCORE_RING[ring_index(b, h) % len(SCORE_RING)]
             scores[b, h] = bank(number, [P, BANK])
+
+        def score_columns(b, h, first, last):
             rows = slice(b * P, (b + 1) * P)
-            cols = slice(h * BANK, (h + 1) * BANK)
+            cols = slice(h * BANK + first, h * BANK + last)
             for g in range(PASSES):
                 nc.tensor.matmul_mx(
-                    out=scores[b, h][:],
+                    out=scores[b, h][:, first:last],
                     lhsT=nf_codes[:, g, rows].bitcast(FP8X4),
                     lhsT_scale=nf_scales[:, g, rows],
                     rhs=nf_codes[:, g, cols].bitcast(FP8X4),
@@ -232,6 +214,10 @@ def tile_custommodel_pa_kernel(tc, frame_embeddings, tau_global_prime, out):
                     start=(g == 0),
                     stop=(g == PASSES - 1),
                 )
+
+        def score_matmuls(b, h):
+            open_scores(b, h)
+            score_columns(b, h, 0, BANK)
 
         def half_maximum(b, h):
             nc.vector.reduce_max(out=half_max[:, b, h : h + 1], in_=scores[b, h][:], axis=AXIS.X)
@@ -355,69 +341,78 @@ def tile_custommodel_pa_kernel(tc, frame_embeddings, tau_global_prime, out):
 
         vector_copy = nc.vector.tensor_copy
         scalar_copy = nc.scalar.copy
+        quarter = BANK // 4
         middle = BANK // 2
 
         sum_of_squares(0)
         sum_of_squares(1)
         sum_of_squares(2)
+        sum_of_squares(3)
         roots(0)
-        regroup_f(0, vector_copy, last=middle)
+        sum_of_squares(4)
+        roots(1)
         add_eps(0)
-        regroup_f(0, vector_copy, first=middle)
+        regroup_f(0, vector_copy, last=quarter)
         invert_norms(0)
+        regroup_f(0, vector_copy, first=quarter, last=middle)
         normalise_and_turn(0)
         normalise_and_turn(1)
-        sum_of_squares(3)
-        roots(1)
         add_eps(1)
-        quantise_f(0)
+        regroup_f(0, vector_copy, first=middle)
         invert_norms(1)
-        regroup_f(1, vector_copy)
+        sum_of_squares(5)
+        sum_of_squares(6)
+        roots(2)
+        sum_of_squares(7)
+        group_nf(0, vector_copy)
         normalise_and_turn(2)
         normalise_and_turn(3)
-        sum_of_squares(4)
-        sum_of_squares(5)
-        roots(2)
-        group_nf(0, scalar_copy)
-        group_nf(1, scalar_copy)
         add_eps(2)
-        regroup_f(2, vector_copy, last=middle)
+        roots(3)
+        group_nf(1, scalar_copy)
+        group_nf(2, scalar_copy)
+        group_nf(3, scalar_copy)
         invert_norms(2)
-        quantise_nf(0, 0)
         normalise_and_turn(4)
         normalise_and_turn(5)
-        quantise_nf(0, 1)
-        quantise_f(1)
-        group_nf(2, vector_copy)
-        sum_of_squares(6)
-        sum_of_squares(7)
-        roots(3)
         add_eps(3)
+        quantise_f(0)
         invert_norms(3)
-        warm_up(3)
+        quantise_nf(0, 0)
         normalise_and_turn(6)
-        group_nf(3, scalar_copy)
         normalise_and_turn(7)
+        quantise_nf(0, 1)
+        regroup_f(1, vector_copy, first=middle)
         quantise_nf(1, 0)
         quantise_nf(1, 1)
-        regroup_f(2, vector_copy, first=middle)
         group_nf(4, scalar_copy)
         group_nf(5, scalar_copy)
-        for b in range(3):
-            score_matmuls(b, 0)
-        quantise_nf(2, 0)
-        quantise_nf(2, 1)
+        nc.scalar.copy(out=late_one[:], in_=one[:])
+        regroup_f_on_gpsimd(2, 256, 384)
+        regroup_f_on_gpsimd(2, 384, 512)
+        regroup_f_on_gpsimd(3, 0, 128)
+        regroup_f_on_gpsimd(3, 128, 256)
+        regroup_f_on_gpsimd(3, 256, 384)
+        regroup_f_on_gpsimd(3, 384, 512)
+        score_matmuls(0, 0)
+        score_matmuls(1, 0)
         group_nf(6, scalar_copy)
         group_nf(7, scalar_copy)
+        quantise_nf(2, 0)
+        quantise_nf(2, 1)
+        open_scores(0, 1)
+        score_columns(0, 1, 0, middle)
+        regroup_f(1, vector_copy, last=middle)
         quantise_nf(3, 0)
         quantise_nf(3, 1)
 
         half_maximum(0, 0)
         load_temperature()
-        nc.scalar.copy(out=late_one[:], in_=one[:])
-        regroup_f_on_gpsimd(3, 4)
-        for b in range(3):
-            score_matmuls(b, 1)
+        regroup_f(2, scalar_copy, last=middle)
+        score_columns(0, 1, middle, BANK)
+        score_matmuls(1, 1)
+        score_matmuls(2, 0)
+        score_matmuls(2, 1)
         score_matmuls(3, 0)
         score_matmuls(3, 1)
         half_maximum(0, 1)
@@ -430,28 +425,28 @@ def tile_custommodel_pa_kernel(tc, frame_embeddings, tau_global_prime, out):
         exponentials(1)
 
         turn_e(0)
-        quantise_f(2)
-        group_e(0, scalar_copy)
         half_maximum(2, 0)
         half_maximum(2, 1)
-        add_half_sums(0)
-        bias_from_maximum(2)
         score_matmuls(4, 0)
-        quantise_e(0)
-        quantise_f(3)
-        invert_sums(0)
+        quantise_f(1)
+        bias_from_maximum(2)
+        group_e(0, scalar_copy)
         score_matmuls(4, 1)
         exponentials(2)
         turn_e(1)
-        group_e(1, scalar_copy)
+        quantise_f(2)
+        quantise_e(0)
+        add_half_sums(0)
+        quantise_f(3)
+        invert_sums(0)
         half_maximum(3, 0)
         half_maximum(3, 1)
+        group_e(1, scalar_copy)
         quantise_e(1)
         bias_from_maximum(3)
         half_maximum(4, 0)
         half_maximum(4, 1)
         weighted_sums_and_divisions(0)
-
         new_scores = {}
         for b in range(PACK, SLABS):
             for h in range(HALVES):

@@ -29,13 +29,13 @@ FLOPS = 2 * 2 * FRAMES * FRAMES * FEATS
 
 NF_BANKS = (4, 5, 6, 7)
 TURN_BANK = 4
-SUM_BANKS = (5, 6)
-SCORE_RING = (0, 1, 2, 3, 7)
-RING_OWNERS = (0, 1, 2, 3, 3)
+SUM_BANKS = (2, 6)
+SCORE_RING = (0, 1, 5, 3, 7)
+RING_OWNERS = (0, 1, 1, 3, 3)
 
 VECTOR_SQUARES = (1, 3)
-LATE = SLABS // 2
-SCALAR_COPIES = (0, 1, 2)
+LATE = 4
+SCALAR_COPIES = (0,1)
 
 
 def tile_custommodel_pa_kernel(tc, frame_embeddings, tau_global_prime, out):
@@ -239,8 +239,12 @@ def tile_custommodel_pa_kernel(tc, frame_embeddings, tau_global_prime, out):
         e_scales = {}
 
         def exponentials(b):
-            e_rows[b] = work.tile([P, FRAMES], BF16, name="e_rows")
             for g in range(HALVES):
+                exponentials_of_half(b, g)
+
+        def exponentials_of_half(b, g):
+                if g == 0:
+                    e_rows[b] = work.tile([P, FRAMES], BF16, name="e_rows")
                 nc.scalar.activation(
                     out=e_rows[b][:, g * BANK : (g + 1) * BANK].rearrange("i (u p v) -> i u p v", u=PAIR, v=PAIR),
                     in_=scores[b, g][:].rearrange("i (u v p) -> i u p v", u=PAIR, v=PAIR),
@@ -324,6 +328,18 @@ def tile_custommodel_pa_kernel(tc, frame_embeddings, tau_global_prime, out):
                 nc.scalar.activation(out=result[:], in_=source[:], func=ACT.Copy, scale=inv_sum[:, b : b + 1])
             nc.sync.dma_start(out=out_rows[:, b // PACK, b % PACK, cols], in_=result[:])
 
+        def divide_quarter(b, n):
+            h, q = divmod(n, 2)
+            width = BANK // 2
+            result = results.tile([P, width], F32, name="result")
+            source = sums[b, h * BANK][:, q * width : (q + 1) * width]
+            if h == 1:
+                nc.vector.tensor_scalar_mul(out=result[:], in0=source, scalar1=inv_sum[:, b : b + 1])
+            else:
+                nc.scalar.activation(out=result[:], in_=source, func=ACT.Copy, scale=inv_sum[:, b : b + 1])
+            cols = slice(n * width, (n + 1) * width)
+            nc.sync.dma_start(out=out_rows[:, b // PACK, b % PACK, cols], in_=result[:])
+
         def weighted_sums_and_divisions(b):
             for h in range(HALVES):
                 weighted_sum(b, slice(h * BANK, (h + 1) * BANK), SUM_BANKS[h])
@@ -352,13 +368,13 @@ def tile_custommodel_pa_kernel(tc, frame_embeddings, tau_global_prime, out):
         sum_of_squares(4)
         roots(1)
         add_eps(0)
-        regroup_f(0, vector_copy, last=quarter)
+        regroup_f(0, vector_copy, first=0, last=128)
         invert_norms(0)
-        regroup_f(0, vector_copy, first=quarter, last=middle)
+        regroup_f(0, vector_copy, first=128, last=256)
         normalise_and_turn(0)
         normalise_and_turn(1)
         add_eps(1)
-        regroup_f(0, vector_copy, first=middle)
+        regroup_f(0, vector_copy, first=256, last=384)
         invert_norms(1)
         sum_of_squares(5)
         sum_of_squares(6)
@@ -368,25 +384,31 @@ def tile_custommodel_pa_kernel(tc, frame_embeddings, tau_global_prime, out):
         normalise_and_turn(2)
         normalise_and_turn(3)
         add_eps(2)
+        regroup_f(0, vector_copy, first=384, last=512)
         roots(3)
         group_nf(1, scalar_copy)
         group_nf(2, scalar_copy)
         group_nf(3, scalar_copy)
         invert_norms(2)
+        regroup_f(1, vector_copy, first=256, last=384)
         normalise_and_turn(4)
         normalise_and_turn(5)
+        regroup_f(1, vector_copy, first=384, last=512)
         add_eps(3)
-        quantise_f(0)
+        regroup_f(1, vector_copy, first=0, last=128)
         invert_norms(3)
         quantise_nf(0, 0)
         normalise_and_turn(6)
         normalise_and_turn(7)
         quantise_nf(0, 1)
-        regroup_f(1, vector_copy, first=middle)
+        regroup_f(1, vector_copy, first=128, last=256)
         quantise_nf(1, 0)
         quantise_nf(1, 1)
         group_nf(4, scalar_copy)
         group_nf(5, scalar_copy)
+        score_matmuls(0, 0)
+        score_matmuls(1, 0)
+        group_nf(6, scalar_copy)
         nc.scalar.copy(out=late_one[:], in_=one[:])
         regroup_f_on_gpsimd(2, 256, 384)
         regroup_f_on_gpsimd(2, 384, 512)
@@ -394,15 +416,12 @@ def tile_custommodel_pa_kernel(tc, frame_embeddings, tau_global_prime, out):
         regroup_f_on_gpsimd(3, 128, 256)
         regroup_f_on_gpsimd(3, 256, 384)
         regroup_f_on_gpsimd(3, 384, 512)
-        score_matmuls(0, 0)
-        score_matmuls(1, 0)
-        group_nf(6, scalar_copy)
         group_nf(7, scalar_copy)
         quantise_nf(2, 0)
         quantise_nf(2, 1)
         open_scores(0, 1)
         score_columns(0, 1, 0, middle)
-        regroup_f(1, vector_copy, last=middle)
+        quantise_f(0)
         quantise_nf(3, 0)
         quantise_nf(3, 1)
 
@@ -422,21 +441,22 @@ def tile_custommodel_pa_kernel(tc, frame_embeddings, tau_global_prime, out):
         half_maximum(1, 1)
         bias_from_maximum(1)
         exponentials(0)
-        exponentials(1)
-
+        exponentials_of_half(1, 0)
         turn_e(0)
         half_maximum(2, 0)
         half_maximum(2, 1)
         score_matmuls(4, 0)
-        quantise_f(1)
+        quantise_f(2)
         bias_from_maximum(2)
         group_e(0, scalar_copy)
+        exponentials_of_half(1, 1)
         score_matmuls(4, 1)
         exponentials(2)
-        turn_e(1)
-        quantise_f(2)
         quantise_e(0)
+        quantise_f(1)
         add_half_sums(0)
+        turn_e(1)
+        score_matmuls(5, 0)
         quantise_f(3)
         invert_sums(0)
         half_maximum(3, 0)
@@ -444,10 +464,9 @@ def tile_custommodel_pa_kernel(tc, frame_embeddings, tau_global_prime, out):
         group_e(1, scalar_copy)
         quantise_e(1)
         bias_from_maximum(3)
-        half_maximum(4, 0)
-        half_maximum(4, 1)
         weighted_sums_and_divisions(0)
         new_scores = {}
+        new_maxima = {2: [(4, 0), (4, 1), (5, 0)], 3: [(5, 1), (6, 0)], 4: [(6, 1), (7, 0)], 5: [(7, 1)]}
         for b in range(PACK, SLABS):
             for h in range(HALVES):
                 n = ring_index(b, h)
@@ -458,6 +477,7 @@ def tile_custommodel_pa_kernel(tc, frame_embeddings, tau_global_prime, out):
         for b in range(2, last):
             sums_ready = b % DUO == 1
             fresh = new_scores.get(b, [])
+            maxima = new_maxima.get(b, [])
             turn_e(b)
             if sums_ready:
                 add_half_sums(b // DUO)
@@ -466,18 +486,23 @@ def tile_custommodel_pa_kernel(tc, frame_embeddings, tau_global_prime, out):
                 score_matmuls(*tile)
             if sums_ready:
                 invert_sums(b // DUO)
-            for tile in fresh[:1]:
+            for tile in maxima[:1]:
                 half_maximum(*tile)
             quantise_e(b)
-            if b + 2 < SLABS:
+            if b + 2 < SLABS and b > 2:
                 bias_from_maximum(b + 2)
-            for tile in fresh[1:]:
+            for tile in maxima[1:]:
                 half_maximum(*tile)
+            if b == 2:
+                bias_from_maximum(b + 2)
             exponentials(b + 1)
             if b + 1 == last:
                 add_half_sums(last // DUO)
             weighted_sums_and_divisions(b - 1)
         invert_sums(last // DUO)
         turn_group_and_quantise_last_e(last)
-        weighted_sums_and_divisions(last - 1)
+        for h in range(HALVES):
+            weighted_sum(last - 1, slice(h * BANK, (h + 1) * BANK), SUM_BANKS[h])
+        for n in range(4):
+            divide_quarter(last - 1, n)
         last_weighted_sums_and_divisions(last)

@@ -410,13 +410,12 @@ def tile_custommodel_pa_kernel(tc, frame_embeddings, tau_global_prime, out):
         score_matmuls(1, 0)
         group_nf(6, scalar_copy)
         nc.scalar.copy(out=late_one[:], in_=one[:])
-        regroup_f_on_gpsimd(2, 256, 384)
-        regroup_f_on_gpsimd(2, 384, 512)
         regroup_f_on_gpsimd(3, 0, 128)
         regroup_f_on_gpsimd(3, 128, 256)
         regroup_f_on_gpsimd(3, 256, 384)
         regroup_f_on_gpsimd(3, 384, 512)
         group_nf(7, scalar_copy)
+        regroup_f(2, vector_copy, first=256, last=512)
         quantise_nf(2, 0)
         quantise_nf(2, 1)
         open_scores(0, 1)

@@ -30,6 +30,8 @@ FLOPS = 2 * 2 * FRAMES * FRAMES * FEATS
 NF_BANKS = (4, 5, 6, 7)
 TURN_BANK = 4
 SUM_BANKS = (2, 6)
+LATE_SUM_BANKS = {5: (3, 2), 6: (0, 6)}
+LAST_BANKS = (1, 5, 3, 2)
 SCORE_RING = (0, 1, 5, 3, 7)
 RING_OWNERS = (0, 1, 1, 3, 3)
 
@@ -342,7 +344,7 @@ def tile_custommodel_pa_kernel(tc, frame_embeddings, tau_global_prime, out):
 
         def weighted_sums_and_divisions(b):
             for h in range(HALVES):
-                weighted_sum(b, slice(h * BANK, (h + 1) * BANK), SUM_BANKS[h])
+                weighted_sum(b, slice(h * BANK, (h + 1) * BANK), LATE_SUM_BANKS.get(b, SUM_BANKS)[h])
             divide_and_store(b, slice(0, BANK), False)
             divide_and_store(b, slice(BANK, FEATS), b >= LATE)
 
@@ -351,7 +353,7 @@ def tile_custommodel_pa_kernel(tc, frame_embeddings, tau_global_prime, out):
             for n in range(4):
                 quarters.append(slice(n * FEATS // 4, (n + 1) * FEATS // 4))
             for n in range(4):
-                weighted_sum(b, quarters[n], SCORE_RING[n])
+                weighted_sum(b, quarters[n], LAST_BANKS[n])
             for n in range(4):
                 divide_and_store(b, quarters[n], n % 2 == 1)
 
@@ -380,28 +382,28 @@ def tile_custommodel_pa_kernel(tc, frame_embeddings, tau_global_prime, out):
         sum_of_squares(6)
         roots(2)
         sum_of_squares(7)
+        regroup_f(0, vector_copy, first=384, last=512)
         group_nf(0, vector_copy)
         normalise_and_turn(2)
         normalise_and_turn(3)
         add_eps(2)
-        regroup_f(0, vector_copy, first=384, last=512)
+        regroup_f(1, vector_copy, first=256, last=384)
         roots(3)
         group_nf(1, scalar_copy)
         group_nf(2, scalar_copy)
         group_nf(3, scalar_copy)
         invert_norms(2)
-        regroup_f(1, vector_copy, first=256, last=384)
+        regroup_f(1, vector_copy, first=384, last=512)
         normalise_and_turn(4)
         normalise_and_turn(5)
-        regroup_f(1, vector_copy, first=384, last=512)
-        add_eps(3)
         regroup_f(1, vector_copy, first=0, last=128)
+        add_eps(3)
+        regroup_f(1, vector_copy, first=128, last=256)
         invert_norms(3)
         quantise_nf(0, 0)
         normalise_and_turn(6)
         normalise_and_turn(7)
         quantise_nf(0, 1)
-        regroup_f(1, vector_copy, first=128, last=256)
         quantise_nf(1, 0)
         quantise_nf(1, 1)
         group_nf(4, scalar_copy)
@@ -501,7 +503,7 @@ def tile_custommodel_pa_kernel(tc, frame_embeddings, tau_global_prime, out):
         invert_sums(last // DUO)
         turn_group_and_quantise_last_e(last)
         for h in range(HALVES):
-            weighted_sum(last - 1, slice(h * BANK, (h + 1) * BANK), SUM_BANKS[h])
+            weighted_sum(last - 1, slice(h * BANK, (h + 1) * BANK), LATE_SUM_BANKS[last - 1][h])
         for n in range(4):
             divide_quarter(last - 1, n)
         last_weighted_sums_and_divisions(last)

@@ -412,12 +412,13 @@ def tile_custommodel_pa_kernel(tc, frame_embeddings, tau_global_prime, out):
         score_matmuls(1, 0)
         group_nf(6, scalar_copy)
         nc.scalar.copy(out=late_one[:], in_=one[:])
+        regroup_f_on_gpsimd(2, 384, 512)
         regroup_f_on_gpsimd(3, 0, 128)
         regroup_f_on_gpsimd(3, 128, 256)
         regroup_f_on_gpsimd(3, 256, 384)
         regroup_f_on_gpsimd(3, 384, 512)
         group_nf(7, scalar_copy)
-        regroup_f(2, vector_copy, first=256, last=512)
+        regroup_f(2, vector_copy, first=256, last=384)
         quantise_nf(2, 0)
         quantise_nf(2, 1)
         open_scores(0, 1)

@@ -166,18 +166,18 @@ def tile_custommodel_pa_kernel(tc, frame_embeddings, tau_global_prime, out):
         def regroup_f(piece, copy, first=0, last=BANK):
             g, h = divmod(piece, HALVES)
             copy(
-                out=f_grouped[piece][:, first:last, :].rearrange("p (c i) t -> p c t i", i=4),
+                out=f_grouped[piece][:, first:last, :].rearrange("p (c i) t -> p c t i", i=8),
                 in_=f_sb[:, g * PACK : (g + 1) * PACK, h * BANK + first : h * BANK + last].rearrange(
-                    "p t (c i) -> p c t i", i=4
+                    "p t (c i) -> p c t i", i=8
                 ),
             )
 
         def regroup_f_on_gpsimd(piece, first=0, last=BANK):
             g, h = divmod(piece, HALVES)
             nc.gpsimd.tensor_scalar(
-                out=f_grouped[piece][:, first:last, :].rearrange("p (c i) t -> p c t i", i=4),
+                out=f_grouped[piece][:, first:last, :].rearrange("p (c i) t -> p c t i", i=8),
                 in0=f_sb[:, g * PACK : (g + 1) * PACK, h * BANK + first : h * BANK + last].rearrange(
-                    "p t (c i) -> p c t i", i=4
+                    "p t (c i) -> p c t i", i=8
                 ),
                 scalar1=late_one[:, 0:1],
                 scalar2=1.0,

from contextlib import ExitStack

import concourse.mybir as mybir
from concourse.masks import make_identity

F32 = mybir.dt.float32
BF16 = mybir.dt.bfloat16
U32 = mybir.dt.uint32
U8 = mybir.dt.uint8
FP8X4 = mybir.dt.float8_e4m3fn_x4
ACT = mybir.ActivationFunctionType
ALU = mybir.AluOpType
AXIS = mybir.AxisListType

P = 128
PACK = 4
PASSES = 2
SLABS = PASSES * PACK
FRAMES = 1024
FEATS = 1024
BANK = 512
HALVES = 2
PAIR = 2
CHUNKS = FEATS // (PAIR * P)
EPS = 1e-6
DUO = 2
DUOS = SLABS // DUO
FLOPS = 2 * 2 * FRAMES * FRAMES * FEATS

NF_BANKS = (4, 5, 6, 7)
TURN_BANK = 4
SUM_BANKS = (2, 6)
LATE_SUM_BANKS = {5: (3, 2), 6: (0, 6)}
LAST_BANKS = (1, 5, 3, 2)
SCORE_RING = (0, 1, 5, 3, 7)
RING_OWNERS = (0, 1, 1, 3, 3)

VECTOR_SQUARES = (1, 3)
LATE = 4
SCALAR_COPIES = (0,1)


def tile_custommodel_pa_kernel(tc, frame_embeddings, tau_global_prime, out):
    nc = tc.nc
    f_rows = frame_embeddings.rearrange("(g p t) d -> p g t d", g=PASSES, t=PACK)
    out_rows = out.rearrange("(g p t) d -> p g t d", g=PASSES, t=PACK)

    with ExitStack() as stack:
        keep = stack.enter_context(tc.tile_pool(name="keep", bufs=1))
        work = stack.enter_context(tc.tile_pool(name="work", bufs=SLABS))
        results = stack.enter_context(tc.tile_pool(name="results", bufs=SLABS * HALVES + 2))
        psum = stack.enter_context(tc.psum_pool(name="psum", bufs=1, reuse_waits="tile"))

        def bank(number, shape):
            return psum.tile(shape, F32, name="bank%d" % number)

        stack.enter_context(tc.manual_schedule())

        f_sb = keep.tile([P, SLABS, FEATS], BF16, align_bytes=64)
        ident = keep.tile([P, P], F32)
        nf_codes = keep.tile([P, PASSES, FRAMES], U32, align_bytes=64)
        nf_scales = keep.tile([P, PASSES, FRAMES], U8, align_bytes=64)
        f_codes = keep.tile([P, PASSES, FEATS], U32, align_bytes=64)
        f_scales = keep.tile([P, PASSES, FEATS], U8, align_bytes=64)
        sumsq = []
        for duo in range(DUOS):
            sumsq.append(keep.tile([P, DUO], F32, name="sumsq%d" % duo))
        half_sum = keep.tile([P, SLABS, HALVES], F32)
        row_sum = keep.tile([P, SLABS], F32)
        inv_tau = keep.tile([P, 1], F32)
        norm = keep.tile([P, SLABS], F32)
        root_of_one = keep.tile([P, 1], F32)
        one = keep.tile([P, 1], F32)
        late_one = keep.tile([P, 1], F32)
        norm_eps = keep.tile([P, SLABS], F32)
        inv_norm = keep.tile([P, SLABS], F32)
        inv_sum = keep.tile([P, SLABS], F32)
        half_max = keep.tile([P, SLABS, HALVES], F32)
        exp_bias = keep.tile([P, SLABS], F32)
        score_scale = keep.tile([P, 1], F32)
        minus_scale = keep.tile([P, 1], F32)
        tau_sb = keep.tile([P, 1], BF16)

        for b in range(SLABS):
            nc.sync.dma_start(out=f_sb[:, b, :], in_=f_rows[:, b // PACK, b % PACK, :])
        nc.sync.dma_start(out=tau_sb[:], in_=tau_global_prime.partition_broadcast(P))
        make_identity(nc, ident[:])
        nc.vector.memset(one[:], 1.0)
        nc.scalar.sqrt(out=root_of_one[:], in_=one[:])

        def load_temperature():
            nc.scalar.activation(out=inv_tau[:], in_=tau_sb[:], func=ACT.Exp, scale=-1.0)

        def scale_temperature():
            nc.vector.tensor_scalar_mul(out=minus_scale[:], in0=inv_tau[:], scalar1=-1.0 / 32.0)
            nc.vector.tensor_scalar_mul(out=score_scale[:], in0=inv_tau[:], scalar1=1.0 / 32.0)

        def sum_of_squares(b):
            total = sumsq[b // DUO][:, b % DUO : b % DUO + 1]
            if b in VECTOR_SQUARES:
                squares = work.tile([P, FEATS], BF16, name="vector_squares")
                nc.vector.scalar_tensor_tensor(
                    out=squares[:],
                    in0=f_sb[:, b, :],
                    scalar=1.0,
                    in1=f_sb[:, b, :],
                    op0=ALU.mult,
                    op1=ALU.mult,
                    accum_out=total,
                )
            else:
                squares = work.tile([P, FEATS], BF16, name="scalar_squares")
                nc.scalar.activation(out=squares[:], in_=f_sb[:, b, :], func=ACT.Square, accum_out=total)

        def roots(duo):
            cols = slice(duo * DUO, (duo + 1) * DUO)
            nc.scalar.sqrt(out=norm[:, cols], in_=sumsq[duo][:])

        def add_eps(duo):
            cols = slice(duo * DUO, (duo + 1) * DUO)
            nc.vector.tensor_scalar_add(out=norm_eps[:, cols], in0=norm[:, cols], scalar1=EPS)

        def invert_norms(duo):
            cols = slice(duo * DUO, (duo + 1) * DUO)
            nc.vector.reciprocal(out=inv_norm[:, cols], in_=norm_eps[:, cols])

        def turn(turned, rows, first_chunk, chunks):
            words = rows[:].bitcast(F32)
            for c in range(chunks):
                q = first_chunk + c
                nc.tensor.transpose(turned[:, c, :], words[:, q * P : (q + 1) * P], ident[:])

        nf_turned = {}
        nf_grouped = {}

        def normalise_and_turn(b):
            nf = work.tile([P, FEATS], BF16, name="nf")
            nc.vector.tensor_scalar_mul(out=nf[:], in0=f_sb[:, b, :], scalar1=inv_norm[:, b : b + 1])
            nf_turned[b] = bank(NF_BANKS[b % len(NF_BANKS)], [P, CHUNKS, P])
            turn(nf_turned[b], nf, 0, CHUNKS)

        def group_nf(b, copy):
            duo, member = divmod(b, DUO)
            if member == 0:
                nf_grouped[duo] = work.tile(
                    [P, PASSES, DUO * P * PACK], BF16, name="nf_grouped", align_bytes=64, bufs=DUOS
                )
            cols = slice(member * P * PACK, (member + 1) * P * PACK)
            copy(
                out=nf_grouped[duo][:, :, cols].bitcast(F32).rearrange("k g (r u) -> k g r u", u=PAIR),
                in_=nf_turned[b][:].rearrange("k (g u) r -> k g r u", u=PAIR),
            )

        def quantise_nf(duo, g):
            cols = slice(duo * DUO * P, (duo + 1) * DUO * P)
            nc.vector.quantize_mx(
                out=nf_codes[:, g, cols].bitcast(FP8X4),
                scales=nf_scales[:, g, cols],
                in_=nf_grouped[duo][:, g, :],
            )

        f_grouped = {}
        for piece in range(PASSES * HALVES):
            f_grouped[piece] = keep.tile([P, BANK, PACK], BF16, name="f_grouped%d" % piece, align_bytes=64)

        def regroup_f(piece, copy, first=0, last=BANK):
            g, h = divmod(piece, HALVES)
            copy(
                out=f_grouped[piece][:, first:last, :].rearrange("p (c i) t -> p c t i", i=8),
                in_=f_sb[:, g * PACK : (g + 1) * PACK, h * BANK + first : h * BANK + last].rearrange(
                    "p t (c i) -> p c t i", i=8
                ),
            )

        def regroup_f_on_gpsimd(piece, first=0, last=BANK):
            g, h = divmod(piece, HALVES)
            nc.gpsimd.tensor_scalar(
                out=f_grouped[piece][:, first:last, :].rearrange("p (c i) t -> p c t i", i=8),
                in0=f_sb[:, g * PACK : (g + 1) * PACK, h * BANK + first : h * BANK + last].rearrange(
                    "p t (c i) -> p c t i", i=8
                ),
                scalar1=late_one[:, 0:1],
                scalar2=1.0,
                op0=ALU.mult,
                op1=ALU.mult,
            )

        def quantise_f(piece):
            g, h = divmod(piece, HALVES)
            cols = slice(h * BANK, (h + 1) * BANK)
            nc.vector.quantize_mx(
                out=f_codes[:, g, cols].bitcast(FP8X4),
                scales=f_scales[:, g, cols],
                in_=f_grouped[piece][:].rearrange("p d t -> p (d t)"),
            )

        scores = {}

        def ring_index(b, h):
            return HALVES * (b - PACK) + h

        def open_scores(b, h):
            number = b + PACK * h if b < PACK else SCORE_RING[ring_index(b, h) % len(SCORE_RING)]
            scores[b, h] = bank(number, [P, BANK])

        def score_columns(b, h, first, last):
            rows = slice(b * P, (b + 1) * P)
            cols = slice(h * BANK + first, h * BANK + last)
            for g in range(PASSES):
                nc.tensor.matmul_mx(
                    out=scores[b, h][:, first:last],
                    lhsT=nf_codes[:, g, rows].bitcast(FP8X4),
                    lhsT_scale=nf_scales[:, g, rows],
                    rhs=nf_codes[:, g, cols].bitcast(FP8X4),
                    rhs_scale=nf_scales[:, g, cols],
                    start=(g == 0),
                    stop=(g == PASSES - 1),
                )

        def score_matmuls(b, h):
            open_scores(b, h)
            score_columns(b, h, 0, BANK)

        def half_maximum(b, h):
            nc.vector.reduce_max(out=half_max[:, b, h : h + 1], in_=scores[b, h][:], axis=AXIS.X)

        def bias_from_maximum(b):
            nc.vector.tensor_scalar(
                out=exp_bias[:, b : b + 1],
                in0=half_max[:, b, 0:1],
                scalar1=half_max[:, b, 1:2],
                scalar2=minus_scale[:, 0:1],
                op0=ALU.max,
                op1=ALU.mult,
            )

        e_rows = {}
        e_turned = {}
        e_grouped = {}
        e_codes = {}
        e_scales = {}

        def exponentials(b):
            for g in range(HALVES):
                exponentials_of_half(b, g)

        def exponentials_of_half(b, g):
                if g == 0:
                    e_rows[b] = work.tile([P, FRAMES], BF16, name="e_rows")
                nc.scalar.activation(
                    out=e_rows[b][:, g * BANK : (g + 1) * BANK].rearrange("i (u p v) -> i u p v", u=PAIR, v=PAIR),
                    in_=scores[b, g][:].rearrange("i (u v p) -> i u p v", u=PAIR, v=PAIR),
                    func=ACT.Exp,
                    bias=exp_bias[:, b : b + 1],
                    scale=score_scale[:, 0:1],
                    accum_out=half_sum[:, b, g : g + 1],
                )

        def add_half_sums(duo):
            slabs = slice(duo * DUO, (duo + 1) * DUO)
            nc.vector.tensor_add(out=row_sum[:, slabs], in0=half_sum[:, slabs, 0], in1=half_sum[:, slabs, 1])

        def invert_sums(duo):
            slabs = slice(duo * DUO, (duo + 1) * DUO)
            nc.vector.reciprocal(out=inv_sum[:, slabs], in_=row_sum[:, slabs])

        def turn_e(b):
            e_turned[b] = bank(TURN_BANK, [P, CHUNKS, P])
            turn(e_turned[b], e_rows[b], 0, CHUNKS)

        def group_e(b, copy):
            e_grouped[b] = work.tile([P, PASSES * P * PACK], BF16, name="e_grouped", align_bytes=64)
            copy(
                out=e_grouped[b][:].bitcast(F32).rearrange("k (g r u) -> k g r u", g=PASSES, u=PAIR),
                in_=e_turned[b][:].rearrange("k (g u) r -> k g r u", u=PAIR),
            )

        def new_e_operand(b):
            e_codes[b] = work.tile([P, PASSES, P], U32, name="e_codes", align_bytes=64)
            e_scales[b] = work.tile([P, PASSES, P], U8, name="e_scales", align_bytes=64)

        def quantise_e(b):
            new_e_operand(b)
            nc.vector.quantize_mx(
                out=e_codes[b][:].rearrange("p g i -> p (g i)").bitcast(FP8X4),
                scales=e_scales[b][:].rearrange("p g i -> p (g i)"),
                in_=e_grouped[b][:],
            )

        def turn_group_and_quantise_last_e(b):
            for g, number in enumerate((TURN_BANK, SCORE_RING[-1])):
                e_turned[b, g] = bank(number, [P, PAIR, P])
                turn(e_turned[b, g], e_rows[b], g * PAIR, PAIR)
            e_grouped[b] = work.tile([P, PASSES * P * PACK], BF16, name="e_grouped", align_bytes=64)
            for g, copy in enumerate((nc.vector.tensor_copy, nc.scalar.copy)):
                cols = slice(g * P * PACK, (g + 1) * P * PACK)
                copy(
                    out=e_grouped[b][:, cols].bitcast(F32).rearrange("k (r u) -> k r u", u=PAIR),
                    in_=e_turned[b, g][:].rearrange("k u r -> k r u"),
                )
            new_e_operand(b)
            for g in range(PASSES):
                nc.vector.quantize_mx(
                    out=e_codes[b][:, g, :].bitcast(FP8X4),
                    scales=e_scales[b][:, g, :],
                    in_=e_grouped[b][:, g * P * PACK : (g + 1) * P * PACK],
                )

        sums = {}

        def weighted_sum(b, cols, number):
            sums[b, cols.start] = bank(number, [P, cols.stop - cols.start])
            for g in range(PASSES):
                nc.tensor.matmul_mx(
                    out=sums[b, cols.start][:],
                    lhsT=e_codes[b][:, g, :].bitcast(FP8X4),
                    lhsT_scale=e_scales[b][:, g, :],
                    rhs=f_codes[:, g, cols].bitcast(FP8X4),
                    rhs_scale=f_scales[:, g, cols],
                    start=(g == 0),
                    stop=(g == PASSES - 1),
                )

        def divide_and_store(b, cols, on_vector):
            result = results.tile([P, cols.stop - cols.start], F32, name="result")
            source = sums[b, cols.start]
            if on_vector:
                nc.vector.tensor_scalar_mul(out=result[:], in0=source[:], scalar1=inv_sum[:, b : b + 1])
            else:
                nc.scalar.activation(out=result[:], in_=source[:], func=ACT.Copy, scale=inv_sum[:, b : b + 1])
            nc.sync.dma_start(out=out_rows[:, b // PACK, b % PACK, cols], in_=result[:])

        def divide_quarter(b, n):
            h, q = divmod(n, 2)
            width = BANK // 2
            result = results.tile([P, width], F32, name="result")
            source = sums[b, h * BANK][:, q * width : (q + 1) * width]
            if h == 1:
                nc.vector.tensor_scalar_mul(out=result[:], in0=source, scalar1=inv_sum[:, b : b + 1])
            else:
                nc.scalar.activation(out=result[:], in_=source, func=ACT.Copy, scale=inv_sum[:, b : b + 1])
            cols = slice(n * width, (n + 1) * width)
            nc.sync.dma_start(out=out_rows[:, b // PACK, b % PACK, cols], in_=result[:])

        def weighted_sums_and_divisions(b):
            for h in range(HALVES):
                weighted_sum(b, slice(h * BANK, (h + 1) * BANK), LATE_SUM_BANKS.get(b, SUM_BANKS)[h])
            divide_and_store(b, slice(0, BANK), False)
            divide_and_store(b, slice(BANK, FEATS), b >= LATE)

        def last_weighted_sums_and_divisions(b):
            quarters = []
            for n in range(4):
                quarters.append(slice(n * FEATS // 4, (n + 1) * FEATS // 4))
            for n in range(4):
                weighted_sum(b, quarters[n], LAST_BANKS[n])
            for n in range(4):
                divide_and_store(b, quarters[n], n % 2 == 1)

        vector_copy = nc.vector.tensor_copy
        scalar_copy = nc.scalar.copy
        quarter = BANK // 4
        middle = BANK // 2

        sum_of_squares(0)
        sum_of_squares(1)
        sum_of_squares(2)
        sum_of_squares(3)
        roots(0)
        sum_of_squares(4)
        roots(1)
        add_eps(0)
        regroup_f(0, vector_copy, first=0, last=128)
        invert_norms(0)
        regroup_f(0, vector_copy, first=128, last=256)
        normalise_and_turn(0)
        normalise_and_turn(1)
        add_eps(1)
        regroup_f(0, vector_copy, first=256, last=384)
        invert_norms(1)
        sum_of_squares(5)
        sum_of_squares(6)
        roots(2)
        sum_of_squares(7)
        regroup_f(0, vector_copy, first=384, last=512)
        group_nf(0, vector_copy)
        normalise_and_turn(2)
        normalise_and_turn(3)
        add_eps(2)
        regroup_f(1, vector_copy, first=256, last=384)
        roots(3)
        group_nf(1, scalar_copy)
        group_nf(2, scalar_copy)
        group_nf(3, scalar_copy)
        invert_norms(2)
        regroup_f(1, vector_copy, first=384, last=512)
        normalise_and_turn(4)
        normalise_and_turn(5)
        regroup_f(1, vector_copy, first=0, last=128)
        add_eps(3)
        regroup_f(1, vector_copy, first=128, last=256)
        invert_norms(3)
        quantise_nf(0, 0)
        normalise_and_turn(6)
        normalise_and_turn(7)
        quantise_nf(0, 1)
        quantise_nf(1, 0)
        quantise_nf(1, 1)
        group_nf(4, scalar_copy)
        group_nf(5, scalar_copy)
        score_matmuls(0, 0)
        score_matmuls(1, 0)
        group_nf(6, scalar_copy)
        nc.scalar.copy(out=late_one[:], in_=one[:])
        regroup_f_on_gpsimd(2, 384, 512)
        regroup_f_on_gpsimd(3, 0, 128)
        regroup_f_on_gpsimd(3, 128, 256)
        regroup_f_on_gpsimd(3, 256, 384)
        regroup_f_on_gpsimd(3, 384, 512)
        group_nf(7, scalar_copy)
        regroup_f(2, vector_copy, first=256, last=384)
        quantise_nf(2, 0)
        quantise_nf(2, 1)
        open_scores(0, 1)
        score_columns(0, 1, 0, middle)
        quantise_f(0)
        quantise_nf(3, 0)
        quantise_nf(3, 1)

        half_maximum(0, 0)
        load_temperature()
        regroup_f(2, scalar_copy, last=middle)
        score_columns(0, 1, middle, BANK)
        score_matmuls(1, 1)
        score_matmuls(2, 0)
        score_matmuls(2, 1)
        score_matmuls(3, 0)
        score_matmuls(3, 1)
        half_maximum(0, 1)
        scale_temperature()
        bias_from_maximum(0)
        half_maximum(1, 0)
        half_maximum(1, 1)
        bias_from_maximum(1)
        exponentials(0)
        exponentials_of_half(1, 0)
        turn_e(0)
        half_maximum(2, 0)
        half_maximum(2, 1)
        score_matmuls(4, 0)
        quantise_f(2)
        bias_from_maximum(2)
        group_e(0, scalar_copy)
        exponentials_of_half(1, 1)
        score_matmuls(4, 1)
        exponentials(2)
        quantise_e(0)
        quantise_f(1)
        add_half_sums(0)
        turn_e(1)
        score_matmuls(5, 0)
        quantise_f(3)
        invert_sums(0)
        half_maximum(3, 0)
        half_maximum(3, 1)
        group_e(1, scalar_copy)
        quantise_e(1)
        bias_from_maximum(3)
        weighted_sums_and_divisions(0)
        new_scores = {}
        new_maxima = {2: [(4, 0), (4, 1), (5, 0)], 3: [(5, 1), (6, 0)], 4: [(6, 1), (7, 0)], 5: [(7, 1)]}
        for b in range(PACK, SLABS):
            for h in range(HALVES):
                n = ring_index(b, h)
                ring = len(SCORE_RING)
                owner = RING_OWNERS[n] if n < ring else PACK + (n - ring) // HALVES
                new_scores.setdefault(owner, []).append((b, h))
        last = SLABS - 1
        for b in range(2, last):
            sums_ready = b % DUO == 1
            fresh = new_scores.get(b, [])
            maxima = new_maxima.get(b, [])
            turn_e(b)
            if sums_ready:
                add_half_sums(b // DUO)
            group_e(b, scalar_copy if b in SCALAR_COPIES else vector_copy)
            for tile in fresh:
                score_matmuls(*tile)
            if sums_ready:
                invert_sums(b // DUO)
            for tile in maxima[:1]:
                half_maximum(*tile)
            quantise_e(b)
            if b + 2 < SLABS and b > 2:
                bias_from_maximum(b + 2)
            for tile in maxima[1:]:
                half_maximum(*tile)
            if b == 2:
                bias_from_maximum(b + 2)
            exponentials(b + 1)
            if b + 1 == last:
                add_half_sums(last // DUO)
            weighted_sums_and_divisions(b - 1)
        invert_sums(last // DUO)
        turn_group_and_quantise_last_e(last)
        for h in range(HALVES):
            weighted_sum(last - 1, slice(h * BANK, (h + 1) * BANK), LATE_SUM_BANKS[last - 1][h])
        for n in range(4):
            divide_quarter(last - 1, n)
        last_weighted_sums_and_divisions(last)
